import numpy as np
import ml_dtypes


def mxq(x, axis, fmt="e4m3"):
    dtype, down = {"e4m3": (ml_dtypes.float8_e4m3fn, 7), "e5m2": (ml_dtypes.float8_e5m2, 14)}[fmt]
    v = np.moveaxis(np.asarray(x, np.float32).astype(ml_dtypes.bfloat16).astype(np.float64), axis, -1)
    blocks = v.reshape(v.shape[:-1] + (-1, 32))
    amax = np.abs(blocks).max(-1, keepdims=True)
    byte = np.maximum(np.where(amax > 0, np.frexp(amax)[1] - 1 + 127, 0) - down, 1)
    scale = np.exp2(byte - 127.0)
    codes = (blocks / scale).astype(np.float32).astype(dtype).astype(np.float64)
    return np.moveaxis((codes * scale).reshape(v.shape), -1, axis)


WIDE = False


def mx_kscale(k):
    if not WIDE:
        return np.ones(k)
    levels = np.array([10, -10, 5, -5, 0])
    a = np.random.permutation(np.resize(levels, k // 512 * 4)).reshape(k // 512, 4)
    idx = np.arange(k)
    return np.exp2(a[idx // 512, idx % 128 // 32])


BF16 = ml_dtypes.bfloat16


def bf(x):
    return np.asarray(x, np.float32).astype(BF16)


def f64(x):
    return np.asarray(x).astype(np.float64)


E2M1 = np.array([0.0, 0.5, 1.0, 1.5, 2.0, 3.0, 4.0, 6.0, -0.0, -0.5, -1.0, -1.5, -2.0, -3.0, -4.0, -6.0])


def pack_weight(w, fmt):
    k, n = w.shape
    w = f64(bf(w)).reshape(k // 32, 32, n)
    amax = np.abs(w).max(1)
    if fmt == "e4m3":
        byte = np.frexp(amax)[1] - 1 + 127 - 7
    else:
        mant, ex = np.frexp(amax / 6.0)
        byte = np.where(mant > 0.5, ex, ex - 1) + 127
    byte = np.clip(np.where(amax > 0, byte, 1), 1, 254)
    scaled = (w * np.exp2(127.0 - byte)[:, None, :]).reshape(k, n).astype(np.float32)
    by_word = np.ascontiguousarray(scaled.reshape(k // 512, 128, 4, n).transpose(0, 1, 3, 2))
    if fmt == "e4m3":
        words = by_word.astype(ml_dtypes.float8_e4m3fn).view(np.uint8)
    else:
        c = by_word.astype(ml_dtypes.float4_e2m1fn).view(np.uint8) & 0xF
        words = c[..., 0::2] | (c[..., 1::2] << 4)
    return np.ascontiguousarray(words), np.ascontiguousarray(byte.astype(np.uint8).reshape(k // 512, 16, n))


def unpack_weight(words, scales, fmt):
    g, p, n, _ = words.shape
    if fmt == "e4m3":
        vals = np.ascontiguousarray(words).view(ml_dtypes.float8_e4m3fn).astype(np.float64)
    else:
        nib = np.empty((g, p, n, 4), np.uint8)
        nib[..., 0::2] = words & 0xF
        nib[..., 1::2] = words >> 4
        vals = E2M1[nib]
    vals = vals * np.repeat(np.exp2(scales.astype(np.float64) - 127.0), 8, axis=1)[..., None]
    return vals.transpose(0, 1, 3, 2).reshape(g * 512, n)


SIZE, DIM, FDIM = 3072, 512, 2048
EPS = 1e-5


def setup_inputs():
    s = mx_kscale(DIM)
    r = np.random.uniform(0.4, 2.0, (SIZE, 1))
    g = np.random.standard_normal((SIZE, DIM))
    words, scales = pack_weight(np.random.standard_normal((DIM, FDIM)) * 1.5 * np.sqrt(np.mean(s * s)) / s[:, None], "e4m3")
    return {"lt_weight": bf(g * s / np.sqrt(np.sum(s * s)) * r),
            "Lambdas_words": words,
            "Lambdas_scales": scales,
            "bias": bf(np.random.uniform(0.0, 2.0 * np.pi, FDIM))}


def reference(lt_weight, Lambdas_words, Lambdas_scales, bias):
    x = f64(lt_weight)
    norms = np.linalg.norm(x, axis=-1, keepdims=True)
    maxnorm = 1.0 - EPS
    e_all = x * np.minimum(1.0, maxnorm / np.maximum(norms, EPS))
    scale = np.sqrt(2.0) / np.sqrt(DIM)
    return scale * np.cos((mxq(e_all, 1, "e4m3") @ unpack_weight(Lambdas_words, Lambdas_scales, "e4m3")) + f64(bias))

@@ -1,0 +1,158 @@
+import math
+from contextlib import ExitStack
+
+import concourse.mybir as mybir
+from concourse.masks import make_identity
+
+BF16 = mybir.dt.bfloat16
+F32 = mybir.dt.float32
+I32 = mybir.dt.int32
+U32 = mybir.dt.uint32
+U8 = mybir.dt.uint8
+FP8X4 = mybir.dt.float8_e4m3fn_x4
+ACT = mybir.ActivationFunctionType
+ALU = mybir.AluOpType
+
+P = 128
+PACK = 4
+SIZE, DIM, FDIM = 3072, 512, 2048
+ROW_TILES = SIZE // P
+GROUP = 4
+BANK_TILES = 2
+N_TILE = 512
+EPS = 1e-5
+MAX_NORM = 1.0 - EPS
+TWO_PI = 2.0 * math.pi
+ROUND_MAGIC = 1.5 * 2.0**23
+OUT_SCALE = math.sqrt(2.0 / DIM)
+FLOPS = 2 * SIZE * DIM * FDIM
+
+
+def tile_rff_kernel(tc, lt_weight, Lambdas_words, Lambdas_scales, bias, out):
+    nc = tc.nc
+    x_rows = lt_weight.rearrange("(p t) k -> p t k", t=ROW_TILES)
+    out_rows = out.rearrange("(p t) n -> p t n", t=ROW_TILES)
+
+    with ExitStack() as ctx:
+        keep = ctx.enter_context(tc.tile_pool(name="keep", bufs=1))
+        small = ctx.enter_context(tc.tile_pool(name="small", bufs=2))
+        stage = ctx.enter_context(tc.tile_pool(name="stage", bufs=2))
+        wide = ctx.enter_context(tc.tile_pool(name="wide", bufs=3))
+        flipped = ctx.enter_context(tc.psum_pool(name="flipped", bufs=2))
+        angles = ctx.enter_context(tc.psum_pool(name="angles", bufs=6))
+
+        x_sb = keep.tile([P, ROW_TILES, DIM], BF16)
+        w_codes = keep.tile([P, FDIM], U32, align_bytes=64)
+        w_plane = keep.tile([P, FDIM], U8, align_bytes=64)
+        bias_bc = keep.tile([P, FDIM], BF16)
+        phase = keep.tile([P, FDIM], F32)
+        ident = keep.tile([P, P], BF16)
+        minus_half = keep.tile([P, GROUP], F32)
+        magic = keep.tile([P, 1], F32)
+        e_codes = keep.tile([P, ROW_TILES, P], U32, align_bytes=64)
+        e_plane = keep.tile([P, ROW_TILES, P], U8, align_bytes=64)
+
+        nc.vector.memset(w_plane[:].bitcast(I32), 0)
+        nc.vector.memset(minus_half[:], -0.5)
+        nc.vector.memset(magic[:], ROUND_MAGIC)
+        make_identity(nc, ident[:])
+
+        nc.sync.dma_start(out=x_sb[:, 0:GROUP, :], in_=x_rows[:, 0:GROUP, :])
+        nc.scalar.dma_start(out=bias_bc[:], in_=bias.partition_broadcast(P))
+        for q in range(4):
+            nc.sync.dma_start(
+                out=w_plane[32 * q : 32 * q + 4, :].bitcast(I32),
+                in_=Lambdas_scales[0, 4 * q : 4 * q + 4, :].bitcast(I32),
+            )
+        nc.sync.dma_start(
+            out=w_codes[:].bitcast(I32),
+            in_=Lambdas_words[0].rearrange("p n t -> p (n t)").bitcast(I32),
+        )
+        for first in range(GROUP, ROW_TILES, GROUP):
+            nc.sync.dma_start(
+                out=x_sb[:, first : first + GROUP, :], in_=x_rows[:, first : first + GROUP, :]
+            )
+
+        nc.vector.tensor_scalar(
+            out=phase[:], in0=bias_bc[:], scalar1=0.5 * math.pi, scalar2=1.0 / TWO_PI,
+            op0=ALU.add, op1=ALU.mult,
+        )
+
+        def prepare_group(first):
+            sumsq = small.tile([P, GROUP], F32)
+            for j in range(GROUP):
+                squares = stage.tile([P, DIM], BF16)
+                nc.scalar.activation(
+                    out=squares[:], in_=x_sb[:, first + j, :], func=ACT.Square,
+                    accum_out=sumsq[:, j : j + 1],
+                )
+            floored = small.tile([P, GROUP], F32)
+            nc.vector.tensor_scalar_max(out=floored[:], in0=sumsq[:], scalar1=EPS * EPS)
+            inv_norm = small.tile([P, GROUP], F32)
+            nc.gpsimd.tensor_tensor(out=inv_norm[:], in0=floored[:], in1=minus_half[:], op=ALU.pow)
+            clip = small.tile([P, GROUP], F32)
+            nc.vector.tensor_scalar(
+                out=clip[:], in0=inv_norm[:], scalar1=MAX_NORM, scalar2=1.0,
+                op0=ALU.mult, op1=ALU.min,
+            )
+            e_sb = stage.tile([P, GROUP, DIM], BF16)
+            for j in range(GROUP):
+                nc.vector.tensor_scalar_mul(
+                    out=e_sb[:, j, :], in0=x_sb[:, first + j, :], scalar1=clip[:, j : j + 1]
+                )
+            grouped = stage.tile([P, GROUP, P, PACK], BF16, align_bytes=64)
+            for half in range(0, GROUP, BANK_TILES):
+                e_t = flipped.tile([P, BANK_TILES, PACK, P], BF16)
+                for j in range(BANK_TILES):
+                    for t in range(PACK):
+                        nc.tensor.transpose(e_t[:, j, t, :], e_sb[:, half + j, t:DIM:PACK], ident[:])
+                nc.scalar.copy(
+                    out=grouped[:, half : half + BANK_TILES, :, :],
+                    in_=e_t[:].rearrange("p j t r -> p j r t"),
+                )
+            nc.vector.quantize_mx(
+                out=e_codes[:, first : first + GROUP, :].rearrange("p j r -> p (j r)").bitcast(FP8X4),
+                scales=e_plane[:, first : first + GROUP, :].rearrange("p j r -> p (j r)"),
+                in_=grouped[:].rearrange("p j r t -> p (j r t)"),
+            )
+
+        def features(t):
+            turns = wide.tile([P, FDIM], F32)
+            for n0 in range(0, FDIM, N_TILE):
+                cols = slice(n0, n0 + N_TILE)
+                angle = angles.tile([P, N_TILE], F32)
+                nc.tensor.matmul_mx(
+                    out=angle[:],
+                    lhsT=e_codes[:, t, :].bitcast(FP8X4),
+                    lhsT_scale=e_plane[:, t, :],
+                    rhs=w_codes[:, cols].bitcast(FP8X4),
+                    rhs_scale=w_plane[:, cols],
+                    start=True,
+                    stop=True,
+                )
+                nc.vector.scalar_tensor_tensor(
+                    out=turns[:, cols], in0=angle[:], scalar=1.0 / TWO_PI, in1=phase[:, cols],
+                    op0=ALU.mult, op1=ALU.add,
+                )
+            shifted = wide.tile([P, FDIM], F32)
+            nc.scalar.activation(out=shifted[:], in_=turns[:], func=ACT.Identity, bias=magic[:])
+            neg_frac = wide.tile([P, FDIM], F32)
+            nc.vector.scalar_tensor_tensor(
+                out=neg_frac[:], in0=shifted[:], scalar=ROUND_MAGIC, in1=turns[:],
+                op0=ALU.subtract, op1=ALU.subtract,
+            )
+            sine = wide.tile([P, FDIM], F32)
+            nc.scalar.activation(out=sine[:], in_=neg_frac[:], func=ACT.Sin, scale=-TWO_PI)
+            result = wide.tile([P, FDIM], F32)
+            nc.gpsimd.tensor_scalar(
+                out=result[:], in0=sine[:], scalar1=OUT_SCALE, scalar2=0.0,
+                op0=ALU.mult, op1=ALU.add,
+            )
+            nc.sync.dma_start(out=out_rows[:, t, :], in_=result[:])
+
+        prepare_group(0)
+        for first in range(0, ROW_TILES, GROUP):
+            if first + GROUP < ROW_TILES:
+                prepare_group(first + GROUP)
+            for t in range(first, first + GROUP):
+                features(t)

@@ -15,10 +15,10 @@ ALU = mybir.AluOpType
 
 P = 128
 PACK = 4
+HALVES = 2
 SIZE, DIM, FDIM = 3072, 512, 2048
 ROW_TILES = SIZE // P
-GROUP = 4
-BANK_TILES = 2
+LOAD_TILES = 4
 N_TILE = 512
 EPS = 1e-5
 MAX_NORM = 1.0 - EPS
@@ -35,9 +35,9 @@ def tile_rff_kernel(tc, lt_weight, Lambdas_words, Lambdas_scales, bias, out):
 
     with ExitStack() as ctx:
         keep = ctx.enter_context(tc.tile_pool(name="keep", bufs=1))
-        small = ctx.enter_context(tc.tile_pool(name="small", bufs=2))
         stage = ctx.enter_context(tc.tile_pool(name="stage", bufs=2))
         wide = ctx.enter_context(tc.tile_pool(name="wide", bufs=3))
+        turns_pool = ctx.enter_context(tc.tile_pool(name="turns_pool", bufs=5))
         flipped = ctx.enter_context(tc.psum_pool(name="flipped", bufs=2))
         angles = ctx.enter_context(tc.psum_pool(name="angles", bufs=6))
 
@@ -46,9 +46,13 @@ def tile_rff_kernel(tc, lt_weight, Lambdas_words, Lambdas_scales, bias, out):
         w_plane = keep.tile([P, FDIM], U8, align_bytes=64)
         bias_bc = keep.tile([P, FDIM], BF16)
         phase = keep.tile([P, FDIM], F32)
-        ident = keep.tile([P, P], BF16)
-        minus_half = keep.tile([P, GROUP], F32)
+        ident = keep.tile([P, P], F32)
+        minus_half = keep.tile([P, 1], F32)
         magic = keep.tile([P, 1], F32)
+        sumsq = keep.tile([P, ROW_TILES], F32)
+        floored = keep.tile([P, ROW_TILES], F32)
+        inv_norm = keep.tile([P, ROW_TILES], F32)
+        clip = keep.tile([P, ROW_TILES], F32)
         e_codes = keep.tile([P, ROW_TILES, P], U32, align_bytes=64)
         e_plane = keep.tile([P, ROW_TILES, P], U8, align_bytes=64)
 
@@ -57,8 +61,8 @@ def tile_rff_kernel(tc, lt_weight, Lambdas_words, Lambdas_scales, bias, out):
         nc.vector.memset(magic[:], ROUND_MAGIC)
         make_identity(nc, ident[:])
 
-        nc.sync.dma_start(out=x_sb[:, 0:GROUP, :], in_=x_rows[:, 0:GROUP, :])
         nc.scalar.dma_start(out=bias_bc[:], in_=bias.partition_broadcast(P))
+        nc.sync.dma_start(out=x_sb[:, 0:LOAD_TILES, :], in_=x_rows[:, 0:LOAD_TILES, :])
         for q in range(4):
             nc.sync.dma_start(
                 out=w_plane[32 * q : 32 * q + 4, :].bitcast(I32),
@@ -68,56 +72,70 @@ def tile_rff_kernel(tc, lt_weight, Lambdas_words, Lambdas_scales, bias, out):
             out=w_codes[:].bitcast(I32),
             in_=Lambdas_words[0].rearrange("p n t -> p (n t)").bitcast(I32),
         )
-        for first in range(GROUP, ROW_TILES, GROUP):
+        for first in range(LOAD_TILES, ROW_TILES, LOAD_TILES):
             nc.sync.dma_start(
-                out=x_sb[:, first : first + GROUP, :], in_=x_rows[:, first : first + GROUP, :]
+                out=x_sb[:, first : first + LOAD_TILES, :],
+                in_=x_rows[:, first : first + LOAD_TILES, :],
             )
 
-        nc.vector.tensor_scalar(
-            out=phase[:], in0=bias_bc[:], scalar1=0.5 * math.pi, scalar2=1.0 / TWO_PI,
-            op0=ALU.add, op1=ALU.mult,
-        )
+        flipped_of = {}
+        grouped_of = {}
+        turns_of = {}
+        shifted_of = {}
+        neg_frac_of = {}
+        sine_of = {}
 
-        def prepare_group(first):
-            sumsq = small.tile([P, GROUP], F32)
-            for j in range(GROUP):
-                squares = stage.tile([P, DIM], BF16)
-                nc.scalar.activation(
-                    out=squares[:], in_=x_sb[:, first + j, :], func=ACT.Square,
-                    accum_out=sumsq[:, j : j + 1],
-                )
-            floored = small.tile([P, GROUP], F32)
-            nc.vector.tensor_scalar_max(out=floored[:], in0=sumsq[:], scalar1=EPS * EPS)
-            inv_norm = small.tile([P, GROUP], F32)
-            nc.gpsimd.tensor_tensor(out=inv_norm[:], in0=floored[:], in1=minus_half[:], op=ALU.pow)
-            clip = small.tile([P, GROUP], F32)
+        def bias_to_phase():
             nc.vector.tensor_scalar(
-                out=clip[:], in0=inv_norm[:], scalar1=MAX_NORM, scalar2=1.0,
+                out=phase[:], in0=bias_bc[:], scalar1=0.5 * math.pi, scalar2=1.0 / TWO_PI,
+                op0=ALU.add, op1=ALU.mult,
+            )
+
+        def sum_squares(t):
+            squares = stage.tile([P, DIM], BF16)
+            nc.scalar.activation(
+                out=squares[:], in_=x_sb[:, t, :], func=ACT.Square, accum_out=sumsq[:, t : t + 1]
+            )
+
+        def floor_norm(t):
+            nc.vector.tensor_scalar_max(
+                out=floored[:, t : t + 1], in0=sumsq[:, t : t + 1], scalar1=EPS * EPS
+            )
+
+        def inverse_norm(t):
+            nc.gpsimd.tensor_tensor(
+                out=inv_norm[:, t : t + 1], in0=floored[:, t : t + 1], in1=minus_half[:], op=ALU.pow
+            )
+
+        def clip_and_flip(t):
+            nc.vector.tensor_scalar(
+                out=clip[:, t : t + 1], in0=inv_norm[:, t : t + 1], scalar1=MAX_NORM, scalar2=1.0,
                 op0=ALU.mult, op1=ALU.min,
             )
-            e_sb = stage.tile([P, GROUP, DIM], BF16)
-            for j in range(GROUP):
-                nc.vector.tensor_scalar_mul(
-                    out=e_sb[:, j, :], in0=x_sb[:, first + j, :], scalar1=clip[:, j : j + 1]
-                )
-            grouped = stage.tile([P, GROUP, P, PACK], BF16, align_bytes=64)
-            for half in range(0, GROUP, BANK_TILES):
-                e_t = flipped.tile([P, BANK_TILES, PACK, P], BF16)
-                for j in range(BANK_TILES):
-                    for t in range(PACK):
-                        nc.tensor.transpose(e_t[:, j, t, :], e_sb[:, half + j, t:DIM:PACK], ident[:])
-                nc.scalar.copy(
-                    out=grouped[:, half : half + BANK_TILES, :, :],
-                    in_=e_t[:].rearrange("p j t r -> p j r t"),
-                )
+            e_sb = stage.tile([P, DIM], BF16)
+            nc.vector.tensor_scalar_mul(out=e_sb[:], in0=x_sb[:, t, :], scalar1=clip[:, t : t + 1])
+            e_words = e_sb[:].bitcast(F32)
+            e_t = flipped.tile([P, HALVES, P], F32)
+            for u in range(HALVES):
+                nc.tensor.transpose(e_t[:, u, :], e_words[:, u : DIM // 2 : HALVES], ident[:])
+            flipped_of[t] = e_t
+
+        def regroup(t):
+            grouped = stage.tile([P, P, PACK], BF16, align_bytes=64)
+            nc.vector.tensor_copy(
+                out=grouped[:].bitcast(F32), in_=flipped_of[t][:].rearrange("p u r -> p r u")
+            )
+            grouped_of[t] = grouped
+
+        def quantise(t):
             nc.vector.quantize_mx(
-                out=e_codes[:, first : first + GROUP, :].rearrange("p j r -> p (j r)").bitcast(FP8X4),
-                scales=e_plane[:, first : first + GROUP, :].rearrange("p j r -> p (j r)"),
-                in_=grouped[:].rearrange("p j r t -> p (j r t)"),
+                out=e_codes[:, t, :].bitcast(FP8X4),
+                scales=e_plane[:, t, :],
+                in_=grouped_of[t][:].rearrange("p r t -> p (r t)"),
             )
 
-        def features(t):
-            turns = wide.tile([P, FDIM], F32)
+        def angles_to_turns(t):
+            turns = turns_pool.tile([P, FDIM], F32)
             for n0 in range(0, FDIM, N_TILE):
                 cols = slice(n0, n0 + N_TILE)
                 angle = angles.tile([P, N_TILE], F32)
@@ -134,25 +152,50 @@ def tile_rff_kernel(tc, lt_weight, Lambdas_words, Lambdas_scales, bias, out):
                     out=turns[:, cols], in0=angle[:], scalar=1.0 / TWO_PI, in1=phase[:, cols],
                     op0=ALU.mult, op1=ALU.add,
                 )
+            turns_of[t] = turns
+
+        def round_turns(t):
             shifted = wide.tile([P, FDIM], F32)
-            nc.scalar.activation(out=shifted[:], in_=turns[:], func=ACT.Identity, bias=magic[:])
+            nc.scalar.activation(out=shifted[:], in_=turns_of[t][:], func=ACT.Identity, bias=magic[:])
+            shifted_of[t] = shifted
+
+        def fraction(t):
             neg_frac = wide.tile([P, FDIM], F32)
             nc.vector.scalar_tensor_tensor(
-                out=neg_frac[:], in0=shifted[:], scalar=ROUND_MAGIC, in1=turns[:],
+                out=neg_frac[:], in0=shifted_of[t][:], scalar=ROUND_MAGIC, in1=turns_of[t][:],
                 op0=ALU.subtract, op1=ALU.subtract,
             )
-            sine = wide.tile([P, FDIM], F32)
-            nc.scalar.activation(out=sine[:], in_=neg_frac[:], func=ACT.Sin, scale=-TWO_PI)
-            result = wide.tile([P, FDIM], F32)
+            neg_frac_of[t] = neg_frac
+
+        def sine(t):
+            sin_t = wide.tile([P, FDIM], F32)
+            nc.scalar.activation(out=sin_t[:], in_=neg_frac_of[t][:], func=ACT.Sin, scale=-TWO_PI)
+            sine_of[t] = sin_t
+
+        def scale_and_store(t):
+            home = turns_of[t + 1] if t + 1 < ROW_TILES else sine_of[t]
             nc.gpsimd.tensor_scalar(
-                out=result[:], in0=sine[:], scalar1=OUT_SCALE, scalar2=0.0,
+                out=home[:], in0=sine_of[t][:], scalar1=OUT_SCALE, scalar2=0.0,
                 op0=ALU.mult, op1=ALU.add,
             )
-            nc.sync.dma_start(out=out_rows[:, t, :], in_=result[:])
+            nc.sync.dma_start(out=out_rows[:, t, :], in_=home[:])
 
-        prepare_group(0)
-        for first in range(0, ROW_TILES, GROUP):
-            if first + GROUP < ROW_TILES:
-                prepare_group(first + GROUP)
-            for t in range(first, first + GROUP):
-                features(t)
+        def run(stage_of, t):
+            if 0 <= t < ROW_TILES:
+                stage_of(t)
+
+        with tc.manual_schedule():
+            for k in range(-4, ROW_TILES + 3):
+                if k == 0:
+                    bias_to_phase()
+                run(inverse_norm, k + 2)
+                run(angles_to_turns, k)
+                run(scale_and_store, k - 3)
+                run(sum_squares, k + 4)
+                run(sine, k - 2)
+                run(round_turns, k)
+                run(regroup, k + 1)
+                run(floor_norm, k + 3)
+                run(clip_and_flip, k + 2)
+                run(quantise, k + 1)
+                run(fraction, k - 1)

@@ -20,6 +20,8 @@ SIZE, DIM, FDIM = 3072, 512, 2048
 ROW_TILES = SIZE // P
 LOAD_TILES = 4
 N_TILE = 512
+GPSIMD_EVERY = 3
+LAST = ROW_TILES - 1
 EPS = 1e-5
 MAX_NORM = 1.0 - EPS
 TWO_PI = 2.0 * math.pi
@@ -44,11 +46,14 @@ def tile_rff_kernel(tc, lt_weight, Lambdas_words, Lambdas_scales, bias, out):
         x_sb = keep.tile([P, ROW_TILES, DIM], BF16)
         w_codes = keep.tile([P, FDIM], U32, align_bytes=64)
         w_plane = keep.tile([P, FDIM], U8, align_bytes=64)
-        bias_bc = keep.tile([P, FDIM], BF16)
+        bias_rows = keep.tile([P, FDIM], BF16)
+        ones = keep.tile([P, P], BF16)
         phase = keep.tile([P, FDIM], F32)
         ident = keep.tile([P, P], F32)
         minus_half = keep.tile([P, 1], F32)
         magic = keep.tile([P, 1], F32)
+        quarter = keep.tile([P, 1], F32)
+        warm = keep.tile([P, 1], F32)
         sumsq = keep.tile([P, ROW_TILES], F32)
         floored = keep.tile([P, ROW_TILES], F32)
         inv_norm = keep.tile([P, ROW_TILES], F32)
@@ -56,12 +61,16 @@ def tile_rff_kernel(tc, lt_weight, Lambdas_words, Lambdas_scales, bias, out):
         e_codes = keep.tile([P, ROW_TILES, P], U32, align_bytes=64)
         e_plane = keep.tile([P, ROW_TILES, P], U8, align_bytes=64)
 
+        nc.vector.memset(bias_rows[:], 0.0)
         nc.vector.memset(w_plane[:].bitcast(I32), 0)
+        nc.vector.memset(quarter[:], 0.25)
+        nc.vector.memset(ones[:], 1.0)
         nc.vector.memset(minus_half[:], -0.5)
         nc.vector.memset(magic[:], ROUND_MAGIC)
         make_identity(nc, ident[:])
 
-        nc.scalar.dma_start(out=bias_bc[:], in_=bias.partition_broadcast(P))
+        nc.scalar.dma_start(out=bias_rows[0:1, :], in_=bias.unsqueeze(0))
+        nc.scalar.activation(out=warm[:], in_=quarter[:], func=ACT.Sin)
         nc.sync.dma_start(out=x_sb[:, 0:LOAD_TILES, :], in_=x_rows[:, 0:LOAD_TILES, :])
         for q in range(4):
             nc.sync.dma_start(
@@ -85,11 +94,24 @@ def tile_rff_kernel(tc, lt_weight, Lambdas_words, Lambdas_scales, bias, out):
         neg_frac_of = {}
         sine_of = {}
 
-        def bias_to_phase():
-            nc.vector.tensor_scalar(
-                out=phase[:], in0=bias_bc[:], scalar1=0.5 * math.pi, scalar2=1.0 / TWO_PI,
-                op0=ALU.add, op1=ALU.mult,
+        def blocks_of(t):
+            width = N_TILE if t == LAST else FDIM
+            return [slice(n0, n0 + width) for n0 in range(0, FDIM, width)]
+
+        bias_everywhere = []
+        for n0 in range(0, FDIM, N_TILE):
+            spread = angles.tile([P, N_TILE], F32, tag="angle")
+            nc.tensor.matmul(
+                out=spread[:], lhsT=ones[:], rhs=bias_rows[:, n0 : n0 + N_TILE], start=True, stop=True
             )
+            bias_everywhere.append(spread)
+
+        def bias_to_phase():
+            for j, spread in enumerate(bias_everywhere):
+                nc.scalar.activation(
+                    out=phase[:, j * N_TILE : (j + 1) * N_TILE], in_=spread[:], func=ACT.Identity,
+                    scale=1.0 / TWO_PI, bias=quarter[:],
+                )
 
         def sum_squares(t):
             squares = stage.tile([P, DIM], BF16)
@@ -122,7 +144,7 @@ def tile_rff_kernel(tc, lt_weight, Lambdas_words, Lambdas_scales, bias, out):
 
         def regroup(t):
             grouped = stage.tile([P, P, PACK], BF16, align_bytes=64)
-            nc.vector.tensor_copy(
+            nc.scalar.copy(
                 out=grouped[:].bitcast(F32), in_=flipped_of[t][:].rearrange("p u r -> p r u")
             )
             grouped_of[t] = grouped
@@ -156,7 +178,15 @@ def tile_rff_kernel(tc, lt_weight, Lambdas_words, Lambdas_scales, bias, out):
 
         def round_turns(t):
             shifted = wide.tile([P, FDIM], F32)
-            nc.scalar.activation(out=shifted[:], in_=turns_of[t][:], func=ACT.Identity, bias=magic[:])
+            if t % GPSIMD_EVERY == GPSIMD_EVERY - 1:
+                nc.gpsimd.tensor_scalar(
+                    out=shifted[:], in0=turns_of[t][:], scalar1=1.0, scalar2=ROUND_MAGIC,
+                    op0=ALU.mult, op1=ALU.add,
+                )
+            else:
+                nc.scalar.activation(
+                    out=shifted[:], in_=turns_of[t][:], func=ACT.Identity, bias=magic[:]
+                )
             shifted_of[t] = shifted
 
         def fraction(t):
@@ -169,16 +199,32 @@ def tile_rff_kernel(tc, lt_weight, Lambdas_words, Lambdas_scales, bias, out):
 
         def sine(t):
             sin_t = wide.tile([P, FDIM], F32)
-            nc.scalar.activation(out=sin_t[:], in_=neg_frac_of[t][:], func=ACT.Sin, scale=-TWO_PI)
+            for cols in blocks_of(t):
+                nc.scalar.activation(
+                    out=sin_t[:, cols], in_=neg_frac_of[t][:, cols], func=ACT.Sin, scale=-TWO_PI
+                )
             sine_of[t] = sin_t
 
         def scale_and_store(t):
-            home = turns_of[t + 1] if t + 1 < ROW_TILES else sine_of[t]
+            home = turns_of[t + 1]
             nc.gpsimd.tensor_scalar(
                 out=home[:], in0=sine_of[t][:], scalar1=OUT_SCALE, scalar2=0.0,
                 op0=ALU.mult, op1=ALU.add,
             )
             nc.sync.dma_start(out=out_rows[:, t, :], in_=home[:])
+
+        def scale_and_store_last(t):
+            for cols in blocks_of(t):
+                nc.vector.tensor_scalar_mul(
+                    out=sine_of[t][:, cols], in0=sine_of[t][:, cols], scalar1=OUT_SCALE
+                )
+                nc.sync.dma_start(out=out_rows[:, t, cols], in_=sine_of[t][:, cols])
+
+        def finish(t):
+            if t < LAST:
+                scale_and_store(t)
+            else:
+                scale_and_store_last(t)
 
         def run(stage_of, t):
             if 0 <= t < ROW_TILES:
@@ -190,11 +236,11 @@ def tile_rff_kernel(tc, lt_weight, Lambdas_words, Lambdas_scales, bias, out):
                     bias_to_phase()
                 run(inverse_norm, k + 2)
                 run(angles_to_turns, k)
-                run(scale_and_store, k - 3)
+                run(finish, k - 3)
                 run(sum_squares, k + 4)
+                run(regroup, k + 1)
                 run(sine, k - 2)
                 run(round_turns, k)
-                run(regroup, k + 1)
                 run(floor_norm, k + 3)
                 run(clip_and_flip, k + 2)
                 run(quantise, k + 1)

@@ -19,9 +19,11 @@ HALVES = 2
 SIZE, DIM, FDIM = 3072, 512, 2048
 ROW_TILES = SIZE // P
 LOAD_TILES = 4
+GROUP = 4
 N_TILE = 512
-GPSIMD_EVERY = 3
-LAST = ROW_TILES - 1
+SCALAR_COLS = 128
+TAIL_FROM = ROW_TILES - 3
+SQUARES_LEAD = 7
 EPS = 1e-5
 MAX_NORM = 1.0 - EPS
 TWO_PI = 2.0 * math.pi
@@ -50,7 +52,7 @@ def tile_rff_kernel(tc, lt_weight, Lambdas_words, Lambdas_scales, bias, out):
         ones = keep.tile([P, P], BF16)
         phase = keep.tile([P, FDIM], F32)
         ident = keep.tile([P, P], F32)
-        minus_half = keep.tile([P, 1], F32)
+        minus_half = keep.tile([P, GROUP], F32)
         magic = keep.tile([P, 1], F32)
         quarter = keep.tile([P, 1], F32)
         warm = keep.tile([P, 1], F32)
@@ -95,7 +97,7 @@ def tile_rff_kernel(tc, lt_weight, Lambdas_words, Lambdas_scales, bias, out):
         sine_of = {}
 
         def blocks_of(t):
-            width = N_TILE if t == LAST else FDIM
+            width = N_TILE if t >= TAIL_FROM else FDIM
             return [slice(n0, n0 + width) for n0 in range(0, FDIM, width)]
 
         bias_everywhere = []
@@ -119,21 +121,24 @@ def tile_rff_kernel(tc, lt_weight, Lambdas_words, Lambdas_scales, bias, out):
                 out=squares[:], in_=x_sb[:, t, :], func=ACT.Square, accum_out=sumsq[:, t : t + 1]
             )
 
-        def floor_norm(t):
-            nc.vector.tensor_scalar_max(
-                out=floored[:, t : t + 1], in0=sumsq[:, t : t + 1], scalar1=EPS * EPS
+        def floor_norms(first):
+            some = slice(first, first + GROUP)
+            nc.vector.tensor_scalar_max(out=floored[:, some], in0=sumsq[:, some], scalar1=EPS * EPS)
+
+        def inverse_norms(first):
+            some = slice(first, first + GROUP)
+            nc.gpsimd.tensor_tensor(
+                out=inv_norm[:, some], in0=floored[:, some], in1=minus_half[:], op=ALU.pow
             )
 
-        def inverse_norm(t):
-            nc.gpsimd.tensor_tensor(
-                out=inv_norm[:, t : t + 1], in0=floored[:, t : t + 1], in1=minus_half[:], op=ALU.pow
+        def clip_factors(first):
+            some = slice(first, first + GROUP)
+            nc.vector.tensor_scalar(
+                out=clip[:, some], in0=inv_norm[:, some], scalar1=MAX_NORM, scalar2=1.0,
+                op0=ALU.mult, op1=ALU.min,
             )
 
         def clip_and_flip(t):
-            nc.vector.tensor_scalar(
-                out=clip[:, t : t + 1], in0=inv_norm[:, t : t + 1], scalar1=MAX_NORM, scalar2=1.0,
-                op0=ALU.mult, op1=ALU.min,
-            )
             e_sb = stage.tile([P, DIM], BF16)
             nc.vector.tensor_scalar_mul(out=e_sb[:], in0=x_sb[:, t, :], scalar1=clip[:, t : t + 1])
             e_words = e_sb[:].bitcast(F32)
@@ -144,7 +149,7 @@ def tile_rff_kernel(tc, lt_weight, Lambdas_words, Lambdas_scales, bias, out):
 
         def regroup(t):
             grouped = stage.tile([P, P, PACK], BF16, align_bytes=64)
-            nc.scalar.copy(
+            nc.vector.tensor_copy(
                 out=grouped[:].bitcast(F32), in_=flipped_of[t][:].rearrange("p u r -> p r u")
             )
             grouped_of[t] = grouped
@@ -178,15 +183,7 @@ def tile_rff_kernel(tc, lt_weight, Lambdas_words, Lambdas_scales, bias, out):
 
         def round_turns(t):
             shifted = wide.tile([P, FDIM], F32)
-            if t % GPSIMD_EVERY == GPSIMD_EVERY - 1:
-                nc.gpsimd.tensor_scalar(
-                    out=shifted[:], in0=turns_of[t][:], scalar1=1.0, scalar2=ROUND_MAGIC,
-                    op0=ALU.mult, op1=ALU.add,
-                )
-            else:
-                nc.scalar.activation(
-                    out=shifted[:], in_=turns_of[t][:], func=ACT.Identity, bias=magic[:]
-                )
+            nc.scalar.activation(out=shifted[:], in_=turns_of[t][:], func=ACT.Identity, bias=magic[:])
             shifted_of[t] = shifted
 
         def fraction(t):
@@ -207,13 +204,15 @@ def tile_rff_kernel(tc, lt_weight, Lambdas_words, Lambdas_scales, bias, out):
 
         def scale_and_store(t):
             home = turns_of[t + 1]
+            split = FDIM - SCALAR_COLS
             nc.gpsimd.tensor_scalar(
-                out=home[:], in0=sine_of[t][:], scalar1=OUT_SCALE, scalar2=0.0,
+                out=home[:, :split], in0=sine_of[t][:, :split], scalar1=OUT_SCALE, scalar2=0.0,
                 op0=ALU.mult, op1=ALU.add,
             )
+            nc.scalar.mul(out=home[:, split:], in_=sine_of[t][:, split:], mul=OUT_SCALE)
             nc.sync.dma_start(out=out_rows[:, t, :], in_=home[:])
 
-        def scale_and_store_last(t):
+        def scale_and_store_at_the_end(t):
             for cols in blocks_of(t):
                 nc.vector.tensor_scalar_mul(
                     out=sine_of[t][:, cols], in0=sine_of[t][:, cols], scalar1=OUT_SCALE
@@ -221,27 +220,32 @@ def tile_rff_kernel(tc, lt_weight, Lambdas_words, Lambdas_scales, bias, out):
                 nc.sync.dma_start(out=out_rows[:, t, cols], in_=sine_of[t][:, cols])
 
         def finish(t):
-            if t < LAST:
+            if t < TAIL_FROM:
                 scale_and_store(t)
             else:
-                scale_and_store_last(t)
+                scale_and_store_at_the_end(t)
 
         def run(stage_of, t):
             if 0 <= t < ROW_TILES:
                 stage_of(t)
 
+        def run_group(stage_of, first):
+            if first % GROUP == 0:
+                run(stage_of, first)
+
         with tc.manual_schedule():
-            for k in range(-4, ROW_TILES + 3):
-                if k == 0:
+            for k in range(-SQUARES_LEAD, ROW_TILES + 3):
+                if k == GROUP - SQUARES_LEAD:
                     bias_to_phase()
-                run(inverse_norm, k + 2)
+                run_group(inverse_norms, k + 2)
                 run(angles_to_turns, k)
                 run(finish, k - 3)
-                run(sum_squares, k + 4)
-                run(regroup, k + 1)
+                run(sum_squares, k + SQUARES_LEAD)
                 run(sine, k - 2)
                 run(round_turns, k)
-                run(floor_norm, k + 3)
+                run(regroup, k + 1)
+                run_group(floor_norms, k + 3)
+                run_group(clip_factors, k + 2)
                 run(clip_and_flip, k + 2)
                 run(quantise, k + 1)
                 run(fraction, k - 1)

@@ -203,7 +203,7 @@ def tile_rff_kernel(tc, lt_weight, Lambdas_words, Lambdas_scales, bias, out):
             sine_of[t] = sin_t
 
         def scale_and_store(t):
-            home = turns_of[t + 1]
+            home = wide.tile([P, FDIM], F32)
             split = FDIM - SCALAR_COLS
             nc.gpsimd.tensor_scalar(
                 out=home[:, :split], in0=sine_of[t][:, :split], scalar1=OUT_SCALE, scalar2=0.0,

@@ -21,7 +21,6 @@ ROW_TILES = SIZE // P
 LOAD_TILES = 4
 GROUP = 4
 N_TILE = 512
-SCALAR_COLS = 128
 TAIL_FROM = ROW_TILES - 3
 SQUARES_LEAD = 7
 EPS = 1e-5
@@ -204,12 +203,10 @@ def tile_rff_kernel(tc, lt_weight, Lambdas_words, Lambdas_scales, bias, out):
 
         def scale_and_store(t):
             home = wide.tile([P, FDIM], F32)
-            split = FDIM - SCALAR_COLS
             nc.gpsimd.tensor_scalar(
-                out=home[:, :split], in0=sine_of[t][:, :split], scalar1=OUT_SCALE, scalar2=0.0,
+                out=home[:], in0=sine_of[t][:], scalar1=OUT_SCALE, scalar2=0.0,
                 op0=ALU.mult, op1=ALU.add,
             )
-            nc.scalar.mul(out=home[:, split:], in_=sine_of[t][:, split:], mul=OUT_SCALE)
             nc.sync.dma_start(out=out_rows[:, t, :], in_=home[:])
 
         def scale_and_store_at_the_end(t):

@@ -148,9 +148,8 @@ def tile_rff_kernel(tc, lt_weight, Lambdas_words, Lambdas_scales, bias, out):
 
         def regroup(t):
             grouped = stage.tile([P, P, PACK], BF16, align_bytes=64)
-            nc.vector.tensor_copy(
-                out=grouped[:].bitcast(F32), in_=flipped_of[t][:].rearrange("p u r -> p r u")
-            )
+            copy_words = nc.scalar.copy if t % 2 == 0 else nc.vector.tensor_copy
+            copy_words(out=grouped[:].bitcast(F32), in_=flipped_of[t][:].rearrange("p u r -> p r u"))
             grouped_of[t] = grouped
 
         def quantise(t):
@@ -237,10 +236,10 @@ def tile_rff_kernel(tc, lt_weight, Lambdas_words, Lambdas_scales, bias, out):
                 run_group(inverse_norms, k + 2)
                 run(angles_to_turns, k)
                 run(finish, k - 3)
+                run(regroup, k + 1)
                 run(sum_squares, k + SQUARES_LEAD)
                 run(sine, k - 2)
                 run(round_turns, k)
-                run(regroup, k + 1)
                 run_group(floor_norms, k + 3)
                 run_group(clip_factors, k + 2)
                 run(clip_and_flip, k + 2)

@@ -148,8 +148,7 @@ def tile_rff_kernel(tc, lt_weight, Lambdas_words, Lambdas_scales, bias, out):
 
         def regroup(t):
             grouped = stage.tile([P, P, PACK], BF16, align_bytes=64)
-            copy_words = nc.scalar.copy if t % 2 == 0 else nc.vector.tensor_copy
-            copy_words(out=grouped[:].bitcast(F32), in_=flipped_of[t][:].rearrange("p u r -> p r u"))
+            nc.scalar.copy(out=grouped[:].bitcast(F32), in_=flipped_of[t][:].rearrange("p u r -> p r u"))
             grouped_of[t] = grouped
 
         def quantise(t):

@@ -22,7 +22,10 @@ LOAD_TILES = 4
 GROUP = 4
 N_TILE = 512
 TAIL_FROM = ROW_TILES - 3
-SQUARES_LEAD = 7
+SQUARES_LEAD = 10
+HEAD_TILES = 2
+HEAD_STEPS = 3
+EARLY_ROWS = 16
 EPS = 1e-5
 MAX_NORM = 1.0 - EPS
 TWO_PI = 2.0 * math.pi
@@ -72,7 +75,14 @@ def tile_rff_kernel(tc, lt_weight, Lambdas_words, Lambdas_scales, bias, out):
 
         nc.scalar.dma_start(out=bias_rows[0:1, :], in_=bias.unsqueeze(0))
         nc.scalar.activation(out=warm[:], in_=quarter[:], func=ACT.Sin)
-        nc.sync.dma_start(out=x_sb[:, 0:LOAD_TILES, :], in_=x_rows[:, 0:LOAD_TILES, :])
+        def load_rows(first):
+            nc.sync.dma_start(
+                out=x_sb[:, first : first + LOAD_TILES, :],
+                in_=x_rows[:, first : first + LOAD_TILES, :],
+            )
+
+        for first in range(0, EARLY_ROWS, LOAD_TILES):
+            load_rows(first)
         for q in range(4):
             nc.sync.dma_start(
                 out=w_plane[32 * q : 32 * q + 4, :].bitcast(I32),
@@ -82,11 +92,8 @@ def tile_rff_kernel(tc, lt_weight, Lambdas_words, Lambdas_scales, bias, out):
             out=w_codes[:].bitcast(I32),
             in_=Lambdas_words[0].rearrange("p n t -> p (n t)").bitcast(I32),
         )
-        for first in range(LOAD_TILES, ROW_TILES, LOAD_TILES):
-            nc.sync.dma_start(
-                out=x_sb[:, first : first + LOAD_TILES, :],
-                in_=x_rows[:, first : first + LOAD_TILES, :],
-            )
+        for first in range(EARLY_ROWS, ROW_TILES, LOAD_TILES):
+            load_rows(first)
 
         flipped_of = {}
         grouped_of = {}
@@ -120,6 +127,16 @@ def tile_rff_kernel(tc, lt_weight, Lambdas_words, Lambdas_scales, bias, out):
                 out=squares[:], in_=x_sb[:, t, :], func=ACT.Square, accum_out=sumsq[:, t : t + 1]
             )
 
+        def sum_squares_on_vector(t):
+            products = stage.tile([P, DIM], F32)
+            nc.vector.scalar_tensor_tensor(
+                out=products[:], in0=x_sb[:, t, :], scalar=1.0, in1=x_sb[:, t, :],
+                op0=ALU.mult, op1=ALU.mult, accum_out=sumsq[:, t : t + 1],
+            )
+
+        vector_squares = list(range(GROUP, GROUP + 2 * HEAD_STEPS))
+        scalar_squares = [t for t in range(ROW_TILES) if t not in vector_squares]
+
         def floor_norms(first):
             some = slice(first, first + GROUP)
             nc.vector.tensor_scalar_max(out=floored[:, some], in0=sumsq[:, some], scalar1=EPS * EPS)
@@ -148,7 +165,8 @@ def tile_rff_kernel(tc, lt_weight, Lambdas_words, Lambdas_scales, bias, out):
 
         def regroup(t):
             grouped = stage.tile([P, P, PACK], BF16, align_bytes=64)
-            nc.scalar.copy(out=grouped[:].bitcast(F32), in_=flipped_of[t][:].rearrange("p u r -> p r u"))
+            copy_words = nc.vector.tensor_copy if t < HEAD_TILES else nc.scalar.copy
+            copy_words(out=grouped[:].bitcast(F32), in_=flipped_of[t][:].rearrange("p u r -> p r u"))
             grouped_of[t] = grouped
 
         def quantise(t):
@@ -232,11 +250,15 @@ def tile_rff_kernel(tc, lt_weight, Lambdas_words, Lambdas_scales, bias, out):
             for k in range(-SQUARES_LEAD, ROW_TILES + 3):
                 if k == GROUP - SQUARES_LEAD:
                     bias_to_phase()
+                if -HEAD_STEPS <= k < 0:
+                    sum_squares_on_vector(vector_squares[2 * (k + HEAD_STEPS)])
+                    sum_squares_on_vector(vector_squares[2 * (k + HEAD_STEPS) + 1])
                 run_group(inverse_norms, k + 2)
                 run(angles_to_turns, k)
                 run(finish, k - 3)
                 run(regroup, k + 1)
-                run(sum_squares, k + SQUARES_LEAD)
+                if k + SQUARES_LEAD < len(scalar_squares):
+                    sum_squares(scalar_squares[k + SQUARES_LEAD])
                 run(sine, k - 2)
                 run(round_turns, k)
                 run_group(floor_norms, k + 3)

@@ -154,9 +154,15 @@ def tile_rff_kernel(tc, lt_weight, Lambdas_words, Lambdas_scales, bias, out):
                 op0=ALU.mult, op1=ALU.min,
             )
 
+        def clips_on_scalar(t):
+            return t - 2 + SQUARES_LEAD >= len(scalar_squares) and t % 2 == 1
+
         def clip_and_flip(t):
             e_sb = stage.tile([P, DIM], BF16)
-            nc.vector.tensor_scalar_mul(out=e_sb[:], in0=x_sb[:, t, :], scalar1=clip[:, t : t + 1])
+            if clips_on_scalar(t):
+                nc.scalar.activation(out=e_sb[:], in_=x_sb[:, t, :], func=ACT.Copy, scale=clip[:, t : t + 1])
+            else:
+                nc.vector.tensor_scalar_mul(out=e_sb[:], in0=x_sb[:, t, :], scalar1=clip[:, t : t + 1])
             e_words = e_sb[:].bitcast(F32)
             e_t = flipped.tile([P, HALVES, P], F32)
             for u in range(HALVES):
@@ -257,12 +263,15 @@ def tile_rff_kernel(tc, lt_weight, Lambdas_words, Lambdas_scales, bias, out):
                 run(angles_to_turns, k)
                 run(finish, k - 3)
                 run(regroup, k + 1)
+                if clips_on_scalar(k + 2):
+                    run(clip_and_flip, k + 2)
                 if k + SQUARES_LEAD < len(scalar_squares):
                     sum_squares(scalar_squares[k + SQUARES_LEAD])
                 run(sine, k - 2)
                 run(round_turns, k)
                 run_group(floor_norms, k + 3)
                 run_group(clip_factors, k + 2)
-                run(clip_and_flip, k + 2)
+                if not clips_on_scalar(k + 2):
+                    run(clip_and_flip, k + 2)
                 run(quantise, k + 1)
                 run(fraction, k - 1)

@@ -18,18 +18,15 @@ PACK = 4
 HALVES = 2
 SIZE, DIM, FDIM = 3072, 512, 2048
 ROW_TILES = SIZE // P
-LOAD_TILES = 4
 GROUP = 4
-N_TILE = 512
-TAIL_FROM = ROW_TILES - 3
-SQUARES_LEAD = 10
-HEAD_TILES = 2
-HEAD_STEPS = 3
-EARLY_ROWS = 16
+GROUPS = ROW_TILES // GROUP
+BLOCKS = FDIM // P
+UNITS = GROUPS * BLOCKS
+STORE_BLOCKS = 4
+QUARTER = STORE_BLOCKS * P
 EPS = 1e-5
 MAX_NORM = 1.0 - EPS
 TWO_PI = 2.0 * math.pi
-ROUND_MAGIC = 1.5 * 2.0**23
 OUT_SCALE = math.sqrt(2.0 / DIM)
 FLOPS = 2 * SIZE * DIM * FDIM
 
@@ -38,25 +35,25 @@ def tile_rff_kernel(tc, lt_weight, Lambdas_words, Lambdas_scales, bias, out):
     nc = tc.nc
     x_rows = lt_weight.rearrange("(p t) k -> p t k", t=ROW_TILES)
     out_rows = out.rearrange("(p t) n -> p t n", t=ROW_TILES)
+    w_hbm = Lambdas_words[0].rearrange("p n t -> p (n t)").bitcast(I32)
 
     with ExitStack() as ctx:
         keep = ctx.enter_context(tc.tile_pool(name="keep", bufs=1))
-        stage = ctx.enter_context(tc.tile_pool(name="stage", bufs=2))
-        wide = ctx.enter_context(tc.tile_pool(name="wide", bufs=3))
-        turns_pool = ctx.enter_context(tc.tile_pool(name="turns_pool", bufs=5))
+        stage = ctx.enter_context(tc.tile_pool(name="stage", bufs=4))
+        homes = ctx.enter_context(tc.tile_pool(name="homes", bufs=4))
         flipped = ctx.enter_context(tc.psum_pool(name="flipped", bufs=2))
-        angles = ctx.enter_context(tc.psum_pool(name="angles", bufs=6))
+        angles = ctx.enter_context(tc.psum_pool(name="angles", bufs=4))
+        upright = ctx.enter_context(tc.psum_pool(name="upright", bufs=2))
 
         x_sb = keep.tile([P, ROW_TILES, DIM], BF16)
         w_codes = keep.tile([P, FDIM], U32, align_bytes=64)
         w_plane = keep.tile([P, FDIM], U8, align_bytes=64)
-        bias_rows = keep.tile([P, FDIM], BF16)
-        ones = keep.tile([P, P], BF16)
-        phase = keep.tile([P, FDIM], F32)
+        bias_rows = keep.tile([P, P], BF16)
+        phase = keep.tile([P, BLOCKS], F32)
+        phase_rad = keep.tile([P, BLOCKS], F32)
         ident = keep.tile([P, P], F32)
+        ident_bf = keep.tile([P, P], BF16)
         minus_half = keep.tile([P, GROUP], F32)
-        magic = keep.tile([P, 1], F32)
-        quarter = keep.tile([P, 1], F32)
         warm = keep.tile([P, 1], F32)
         sumsq = keep.tile([P, ROW_TILES], F32)
         floored = keep.tile([P, ROW_TILES], F32)
@@ -66,62 +63,42 @@ def tile_rff_kernel(tc, lt_weight, Lambdas_words, Lambdas_scales, bias, out):
         e_plane = keep.tile([P, ROW_TILES, P], U8, align_bytes=64)
 
         nc.vector.memset(bias_rows[:], 0.0)
-        nc.vector.memset(w_plane[:].bitcast(I32), 0)
-        nc.vector.memset(quarter[:], 0.25)
-        nc.vector.memset(ones[:], 1.0)
         nc.vector.memset(minus_half[:], -0.5)
-        nc.vector.memset(magic[:], ROUND_MAGIC)
+        nc.vector.memset(w_plane[:].bitcast(I32), 0)
         make_identity(nc, ident[:])
+        make_identity(nc, ident_bf[:])
 
-        nc.scalar.dma_start(out=bias_rows[0:1, :], in_=bias.unsqueeze(0))
-        nc.scalar.activation(out=warm[:], in_=quarter[:], func=ACT.Sin)
-        def load_rows(first):
+        nc.scalar.dma_start(out=bias_rows[0:BLOCKS, :], in_=bias.rearrange("(j p) -> j p", p=P))
+        nc.scalar.activation(out=warm[:], in_=minus_half[:, 0:1], func=ACT.Sin)
+
+        def load_group(g):
             nc.sync.dma_start(
-                out=x_sb[:, first : first + LOAD_TILES, :],
-                in_=x_rows[:, first : first + LOAD_TILES, :],
+                out=x_sb[:, GROUP * g : GROUP * (g + 1), :], in_=x_rows[:, GROUP * g : GROUP * (g + 1), :]
             )
 
-        for first in range(0, EARLY_ROWS, LOAD_TILES):
-            load_rows(first)
+        load_group(0)
+        load_group(1)
         for q in range(4):
             nc.sync.dma_start(
                 out=w_plane[32 * q : 32 * q + 4, :].bitcast(I32),
                 in_=Lambdas_scales[0, 4 * q : 4 * q + 4, :].bitcast(I32),
             )
-        nc.sync.dma_start(
-            out=w_codes[:].bitcast(I32),
-            in_=Lambdas_words[0].rearrange("p n t -> p (n t)").bitcast(I32),
-        )
-        for first in range(EARLY_ROWS, ROW_TILES, LOAD_TILES):
-            load_rows(first)
+        for n0 in range(0, FDIM, QUARTER):
+            nc.sync.dma_start(out=w_codes[:, n0 : n0 + QUARTER].bitcast(I32), in_=w_hbm[:, n0 : n0 + QUARTER])
+        for g in range(2, GROUPS):
+            load_group(g)
 
+        e_of = {}
         flipped_of = {}
         grouped_of = {}
-        turns_of = {}
-        shifted_of = {}
-        neg_frac_of = {}
+        angle_of = {}
+        whole_of = {}
+        part_of = {}
         sine_of = {}
+        upright_of = {}
+        home_of = {}
 
-        def blocks_of(t):
-            width = N_TILE if t >= TAIL_FROM else FDIM
-            return [slice(n0, n0 + width) for n0 in range(0, FDIM, width)]
-
-        bias_everywhere = []
-        for n0 in range(0, FDIM, N_TILE):
-            spread = angles.tile([P, N_TILE], F32, tag="angle")
-            nc.tensor.matmul(
-                out=spread[:], lhsT=ones[:], rhs=bias_rows[:, n0 : n0 + N_TILE], start=True, stop=True
-            )
-            bias_everywhere.append(spread)
-
-        def bias_to_phase():
-            for j, spread in enumerate(bias_everywhere):
-                nc.scalar.activation(
-                    out=phase[:, j * N_TILE : (j + 1) * N_TILE], in_=spread[:], func=ACT.Identity,
-                    scale=1.0 / TWO_PI, bias=quarter[:],
-                )
-
-        def sum_squares(t):
+        def sum_squares_on_scalar(t):
             squares = stage.tile([P, DIM], BF16)
             nc.scalar.activation(
                 out=squares[:], in_=x_sb[:, t, :], func=ACT.Square, accum_out=sumsq[:, t : t + 1]
@@ -134,44 +111,37 @@ def tile_rff_kernel(tc, lt_weight, Lambdas_words, Lambdas_scales, bias, out):
                 op0=ALU.mult, op1=ALU.mult, accum_out=sumsq[:, t : t + 1],
             )
 
-        vector_squares = list(range(GROUP, GROUP + 2 * HEAD_STEPS))
-        scalar_squares = [t for t in range(ROW_TILES) if t not in vector_squares]
-
-        def floor_norms(first):
-            some = slice(first, first + GROUP)
-            nc.vector.tensor_scalar_max(out=floored[:, some], in0=sumsq[:, some], scalar1=EPS * EPS)
-
-        def inverse_norms(first):
-            some = slice(first, first + GROUP)
+        def clip_factors(g):
+            some = slice(GROUP * g, GROUP * (g + 1))
+            nc.gpsimd.tensor_scalar(
+                out=floored[:, some], in0=sumsq[:, some], scalar1=EPS * EPS, scalar2=0.0,
+                op0=ALU.max, op1=ALU.add,
+            )
             nc.gpsimd.tensor_tensor(
                 out=inv_norm[:, some], in0=floored[:, some], in1=minus_half[:], op=ALU.pow
             )
-
-        def clip_factors(first):
-            some = slice(first, first + GROUP)
-            nc.vector.tensor_scalar(
+            nc.gpsimd.tensor_scalar(
                 out=clip[:, some], in0=inv_norm[:, some], scalar1=MAX_NORM, scalar2=1.0,
                 op0=ALU.mult, op1=ALU.min,
             )
 
-        def clips_on_scalar(t):
-            return t - 2 + SQUARES_LEAD >= len(scalar_squares) and t % 2 == 1
-
-        def clip_and_flip(t):
+        def clip_rows(t, engine):
             e_sb = stage.tile([P, DIM], BF16)
-            if clips_on_scalar(t):
-                nc.scalar.activation(out=e_sb[:], in_=x_sb[:, t, :], func=ACT.Copy, scale=clip[:, t : t + 1])
-            else:
-                nc.vector.tensor_scalar_mul(out=e_sb[:], in0=x_sb[:, t, :], scalar1=clip[:, t : t + 1])
-            e_words = e_sb[:].bitcast(F32)
-            e_t = flipped.tile([P, HALVES, P], F32)
+            engine.tensor_scalar(
+                out=e_sb[:], in0=x_sb[:, t, :], scalar1=clip[:, t : t + 1], scalar2=0.0,
+                op0=ALU.mult, op1=ALU.add,
+            )
+            e_of[t] = e_sb
+
+        def flip(t):
+            e_words = e_of[t][:].bitcast(F32)
+            e_t = flipped.tile([P, HALVES, P], F32, tag="flip")
             for u in range(HALVES):
                 nc.tensor.transpose(e_t[:, u, :], e_words[:, u : DIM // 2 : HALVES], ident[:])
             flipped_of[t] = e_t
 
-        def regroup(t):
+        def regroup(t, copy_words):
             grouped = stage.tile([P, P, PACK], BF16, align_bytes=64)
-            copy_words = nc.vector.tensor_copy if t < HEAD_TILES else nc.scalar.copy
             copy_words(out=grouped[:].bitcast(F32), in_=flipped_of[t][:].rearrange("p u r -> p r u"))
             grouped_of[t] = grouped
 
@@ -182,96 +152,126 @@ def tile_rff_kernel(tc, lt_weight, Lambdas_words, Lambdas_scales, bias, out):
                 in_=grouped_of[t][:].rearrange("p r t -> p (r t)"),
             )
 
-        def angles_to_turns(t):
-            turns = turns_pool.tile([P, FDIM], F32)
-            for n0 in range(0, FDIM, N_TILE):
-                cols = slice(n0, n0 + N_TILE)
-                angle = angles.tile([P, N_TILE], F32)
-                nc.tensor.matmul_mx(
-                    out=angle[:],
-                    lhsT=e_codes[:, t, :].bitcast(FP8X4),
-                    lhsT_scale=e_plane[:, t, :],
-                    rhs=w_codes[:, cols].bitcast(FP8X4),
-                    rhs_scale=w_plane[:, cols],
-                    start=True,
-                    stop=True,
-                )
-                nc.vector.scalar_tensor_tensor(
-                    out=turns[:, cols], in0=angle[:], scalar=1.0 / TWO_PI, in1=phase[:, cols],
-                    op0=ALU.mult, op1=ALU.add,
-                )
-            turns_of[t] = turns
-
-        def round_turns(t):
-            shifted = wide.tile([P, FDIM], F32)
-            nc.scalar.activation(out=shifted[:], in_=turns_of[t][:], func=ACT.Identity, bias=magic[:])
-            shifted_of[t] = shifted
-
-        def fraction(t):
-            neg_frac = wide.tile([P, FDIM], F32)
-            nc.vector.scalar_tensor_tensor(
-                out=neg_frac[:], in0=shifted_of[t][:], scalar=ROUND_MAGIC, in1=turns_of[t][:],
-                op0=ALU.subtract, op1=ALU.subtract,
+        def multiply(u):
+            g, j = divmod(u, BLOCKS)
+            rows = slice(GROUP * g, GROUP * (g + 1))
+            cols = slice(P * j, P * (j + 1))
+            angle = angles.tile([P, GROUP * P], F32)
+            nc.tensor.matmul_mx(
+                out=angle[:],
+                lhsT=w_codes[:, cols].bitcast(FP8X4),
+                lhsT_scale=w_plane[:, cols],
+                rhs=e_codes[:, rows, :].rearrange("p t r -> p (t r)").bitcast(FP8X4),
+                rhs_scale=e_plane[:, rows, :].rearrange("p t r -> p (t r)"),
+                start=True,
+                stop=True,
             )
-            neg_frac_of[t] = neg_frac
+            angle_of[u] = angle
 
-        def sine(t):
-            sin_t = wide.tile([P, FDIM], F32)
-            for cols in blocks_of(t):
-                nc.scalar.activation(
-                    out=sin_t[:, cols], in_=neg_frac_of[t][:, cols], func=ACT.Sin, scale=-TWO_PI
-                )
-            sine_of[t] = sin_t
-
-        def scale_and_store(t):
-            home = wide.tile([P, FDIM], F32)
-            nc.gpsimd.tensor_scalar(
-                out=home[:], in0=sine_of[t][:], scalar1=OUT_SCALE, scalar2=0.0,
+        def whole_turns(u):
+            j = u % BLOCKS
+            whole = stage.tile([P, GROUP * P], I32)
+            nc.vector.tensor_scalar(
+                out=whole[:], in0=angle_of[u][:], scalar1=1.0 / TWO_PI, scalar2=phase[:, j : j + 1],
                 op0=ALU.mult, op1=ALU.add,
             )
-            nc.sync.dma_start(out=out_rows[:, t, :], in_=home[:])
+            whole_of[u] = whole
 
-        def scale_and_store_at_the_end(t):
-            for cols in blocks_of(t):
-                nc.vector.tensor_scalar_mul(
-                    out=sine_of[t][:, cols], in0=sine_of[t][:, cols], scalar1=OUT_SCALE
-                )
-                nc.sync.dma_start(out=out_rows[:, t, cols], in_=sine_of[t][:, cols])
+        def part_turn(u):
+            part = stage.tile([P, GROUP * P], F32)
+            nc.vector.scalar_tensor_tensor(
+                out=part[:], in0=angle_of[u][:], scalar=1.0 / TWO_PI, in1=whole_of[u][:],
+                op0=ALU.mult, op1=ALU.subtract,
+            )
+            part_of[u] = part
 
-        def finish(t):
-            if t < TAIL_FROM:
-                scale_and_store(t)
+        def sine(u):
+            j = u % BLOCKS
+            sin_u = stage.tile([P, GROUP * P], F32)
+            nc.scalar.activation(
+                out=sin_u[:], in_=part_of[u][:], func=ACT.Sin, scale=TWO_PI, bias=phase_rad[:, j : j + 1]
+            )
+            sine_of[u] = sin_u
+
+        def turn_back(u):
+            up = upright.tile([P, GROUP, P], F32)
+            for i in range(GROUP):
+                nc.tensor.transpose(up[:, i, :], sine_of[u][:, P * i : P * (i + 1)], ident[:])
+            upright_of[u] = up
+
+        def scale_and_store(u):
+            g, j = divmod(u, BLOCKS)
+            quarter, b = divmod(j, STORE_BLOCKS)
+            if b == 0:
+                home = homes.tile([P, GROUP, QUARTER], F32)
+                home_of[g, quarter] = home
+            home = home_of[g, quarter]
+            cols = slice(P * b, P * (b + 1))
+            last = u >= UNITS - STORE_BLOCKS
+            if last and b % 2 == 0:
+                nc.vector.tensor_scalar_mul(out=home[:, :, cols], in0=upright_of[u][:], scalar1=OUT_SCALE)
             else:
-                scale_and_store_at_the_end(t)
+                nc.scalar.mul(out=home[:, :, cols], in_=upright_of[u][:], mul=OUT_SCALE)
+            rows = slice(GROUP * g, GROUP * (g + 1))
+            if last:
+                nc.sync.dma_start(out=out_rows[:, rows, P * j : P * (j + 1)], in_=home[:, :, cols])
+            elif b == STORE_BLOCKS - 1:
+                nc.sync.dma_start(
+                    out=out_rows[:, rows, QUARTER * quarter : QUARTER * (quarter + 1)], in_=home[:]
+                )
 
-        def run(stage_of, t):
-            if 0 <= t < ROW_TILES:
-                stage_of(t)
-
-        def run_group(stage_of, first):
-            if first % GROUP == 0:
-                run(stage_of, first)
+        def run(stage_of, u):
+            if 0 <= u < UNITS:
+                stage_of(u)
 
         with tc.manual_schedule():
-            for k in range(-SQUARES_LEAD, ROW_TILES + 3):
-                if k == GROUP - SQUARES_LEAD:
-                    bias_to_phase()
-                if -HEAD_STEPS <= k < 0:
-                    sum_squares_on_vector(vector_squares[2 * (k + HEAD_STEPS)])
-                    sum_squares_on_vector(vector_squares[2 * (k + HEAD_STEPS) + 1])
-                run_group(inverse_norms, k + 2)
-                run(angles_to_turns, k)
-                run(finish, k - 3)
-                run(regroup, k + 1)
-                if clips_on_scalar(k + 2):
-                    run(clip_and_flip, k + 2)
-                if k + SQUARES_LEAD < len(scalar_squares):
-                    sum_squares(scalar_squares[k + SQUARES_LEAD])
+            for t in (0, 1):
+                sum_squares_on_vector(t)
+            for t in (2, 3, 4, 5, 6, 7):
+                sum_squares_on_scalar(t)
+            clip_factors(0)
+
+            bias_columns = flipped.tile([P, P], BF16, tag="flip")
+            nc.tensor.transpose(bias_columns[:], bias_rows[:], ident_bf[:])
+            nc.vector.tensor_scalar(
+                out=phase[:], in0=bias_columns[:, 0:BLOCKS], scalar1=1.0 / TWO_PI, scalar2=0.25,
+                op0=ALU.mult, op1=ALU.add,
+            )
+            nc.vector.tensor_scalar(
+                out=phase_rad[:], in0=bias_columns[:, 0:BLOCKS], scalar1=1.0, scalar2=0.5 * math.pi,
+                op0=ALU.mult, op1=ALU.add,
+            )
+            for t in range(GROUP):
+                clip_rows(t, nc.vector)
+                flip(t)
+            for t in range(GROUP):
+                regroup(t, nc.vector.tensor_copy if t % 2 == 0 else nc.scalar.copy)
+            for t in range(GROUP):
+                quantise(t)
+            clip_factors(1)
+
+            for k in range(-5, UNITS + 4):
+                run(multiply, k + 2)
+                run(turn_back, k - 3)
+                for t in range(GROUP, ROW_TILES):
+                    g, i = divmod(t, GROUP)
+                    begin = BLOCKS * (g - 1) + 4 * i - 5
+                    if g >= 2 and k == BLOCKS * (g - 2) + 2 * i + 1:
+                        if i % 2 == 0:
+                            sum_squares_on_scalar(t)
+                        else:
+                            sum_squares_on_vector(t)
+                    if g >= 2 and i == 0 and k == begin - 2:
+                        clip_factors(g)
+                    if k == begin:
+                        clip_rows(t, nc.gpsimd)
+                    if k == begin + 1:
+                        flip(t)
+                    if k == begin + 2:
+                        regroup(t, nc.scalar.copy)
+                    if k == begin + 3:
+                        quantise(t)
+                run(whole_turns, k)
+                run(part_turn, k - 1)
                 run(sine, k - 2)
-                run(round_turns, k)
-                run_group(floor_norms, k + 3)
-                run_group(clip_factors, k + 2)
-                if not clips_on_scalar(k + 2):
-                    run(clip_and_flip, k + 2)
-                run(quantise, k + 1)
-                run(fraction, k - 1)
+                run(scale_and_store, k - 4)

@@ -20,13 +20,17 @@ SIZE, DIM, FDIM = 3072, 512, 2048
 ROW_TILES = SIZE // P
 GROUP = 4
 GROUPS = ROW_TILES // GROUP
+N_TILE = 512
+ROW_BANKS = 2
+ROW_FEATURES = ROW_BANKS * N_TILE
 BLOCKS = FDIM // P
-UNITS = GROUPS * BLOCKS
-STORE_BLOCKS = 4
-QUARTER = STORE_BLOCKS * P
+SLOT_BLOCKS = (BLOCKS - ROW_FEATURES // P) // GROUP
+HOME_BLOCKS = 4
+TAIL_FROM = ROW_TILES - 2
 EPS = 1e-5
 MAX_NORM = 1.0 - EPS
 TWO_PI = 2.0 * math.pi
+ROUND_MAGIC = 1.5 * 2.0**23
 OUT_SCALE = math.sqrt(2.0 / DIM)
 FLOPS = 2 * SIZE * DIM * FDIM
 
@@ -40,20 +44,25 @@ def tile_rff_kernel(tc, lt_weight, Lambdas_words, Lambdas_scales, bias, out):
     with ExitStack() as ctx:
         keep = ctx.enter_context(tc.tile_pool(name="keep", bufs=1))
         stage = ctx.enter_context(tc.tile_pool(name="stage", bufs=4))
-        homes = ctx.enter_context(tc.tile_pool(name="homes", bufs=4))
-        flipped = ctx.enter_context(tc.psum_pool(name="flipped", bufs=2))
-        angles = ctx.enter_context(tc.psum_pool(name="angles", bufs=4))
+        rounded = ctx.enter_context(tc.tile_pool(name="rounded", bufs=5))
+        homes = ctx.enter_context(tc.tile_pool(name="homes", bufs=3))
+        flipped = ctx.enter_context(tc.psum_pool(name="flipped", bufs=1))
+        angles = ctx.enter_context(tc.psum_pool(name="angles", bufs=5))
         upright = ctx.enter_context(tc.psum_pool(name="upright", bufs=2))
 
         x_sb = keep.tile([P, ROW_TILES, DIM], BF16)
         w_codes = keep.tile([P, FDIM], U32, align_bytes=64)
         w_plane = keep.tile([P, FDIM], U8, align_bytes=64)
         bias_rows = keep.tile([P, P], BF16)
+        bias_row = keep.tile([P, ROW_FEATURES], BF16)
+        ones = keep.tile([P, P], BF16)
+        row_phase = keep.tile([P, ROW_FEATURES], F32)
         phase = keep.tile([P, BLOCKS], F32)
         phase_rad = keep.tile([P, BLOCKS], F32)
         ident = keep.tile([P, P], F32)
         ident_bf = keep.tile([P, P], BF16)
         minus_half = keep.tile([P, GROUP], F32)
+        magic = keep.tile([P, 1], F32)
         warm = keep.tile([P, 1], F32)
         sumsq = keep.tile([P, ROW_TILES], F32)
         floored = keep.tile([P, ROW_TILES], F32)
@@ -65,10 +74,14 @@ def tile_rff_kernel(tc, lt_weight, Lambdas_words, Lambdas_scales, bias, out):
         nc.vector.memset(bias_rows[:], 0.0)
         nc.vector.memset(minus_half[:], -0.5)
         nc.vector.memset(w_plane[:].bitcast(I32), 0)
+        nc.vector.memset(bias_row[:], 0.0)
+        nc.vector.memset(ones[:], 1.0)
+        nc.vector.memset(magic[:], ROUND_MAGIC)
         make_identity(nc, ident[:])
         make_identity(nc, ident_bf[:])
 
         nc.scalar.dma_start(out=bias_rows[0:BLOCKS, :], in_=bias.rearrange("(j p) -> j p", p=P))
+        nc.scalar.dma_start(out=bias_row[0:1, :], in_=bias[0:ROW_FEATURES].unsqueeze(0))
         nc.scalar.activation(out=warm[:], in_=minus_half[:, 0:1], func=ACT.Sin)
 
         def load_group(g):
@@ -76,25 +89,29 @@ def tile_rff_kernel(tc, lt_weight, Lambdas_words, Lambdas_scales, bias, out):
                 out=x_sb[:, GROUP * g : GROUP * (g + 1), :], in_=x_rows[:, GROUP * g : GROUP * (g + 1), :]
             )
 
-        load_group(0)
-        load_group(1)
+        for g in range(3):
+            load_group(g)
         for q in range(4):
             nc.sync.dma_start(
                 out=w_plane[32 * q : 32 * q + 4, :].bitcast(I32),
                 in_=Lambdas_scales[0, 4 * q : 4 * q + 4, :].bitcast(I32),
             )
-        for n0 in range(0, FDIM, QUARTER):
-            nc.sync.dma_start(out=w_codes[:, n0 : n0 + QUARTER].bitcast(I32), in_=w_hbm[:, n0 : n0 + QUARTER])
-        for g in range(2, GROUPS):
+        for n0 in range(0, FDIM, N_TILE):
+            nc.sync.dma_start(out=w_codes[:, n0 : n0 + N_TILE].bitcast(I32), in_=w_hbm[:, n0 : n0 + N_TILE])
+        for g in range(3, GROUPS):
             load_group(g)
 
         e_of = {}
         flipped_of = {}
         grouped_of = {}
-        angle_of = {}
-        whole_of = {}
+        angles_of = {}
+        turns_of = {}
+        shifted_of = {}
         part_of = {}
         sine_of = {}
+        whole_of = {}
+        block_part_of = {}
+        block_sine_of = {}
         upright_of = {}
         home_of = {}
 
@@ -133,9 +150,9 @@ def tile_rff_kernel(tc, lt_weight, Lambdas_words, Lambdas_scales, bias, out):
             )
             e_of[t] = e_sb
 
-        def flip(t):
+        def flip(t, pool, tag):
             e_words = e_of[t][:].bitcast(F32)
-            e_t = flipped.tile([P, HALVES, P], F32, tag="flip")
+            e_t = pool.tile([P, HALVES, P], F32, tag=tag)
             for u in range(HALVES):
                 nc.tensor.transpose(e_t[:, u, :], e_words[:, u : DIM // 2 : HALVES], ident[:])
             flipped_of[t] = e_t
@@ -152,77 +169,141 @@ def tile_rff_kernel(tc, lt_weight, Lambdas_words, Lambdas_scales, bias, out):
                 in_=grouped_of[t][:].rearrange("p r t -> p (r t)"),
             )
 
-        def multiply(u):
-            g, j = divmod(u, BLOCKS)
-            rows = slice(GROUP * g, GROUP * (g + 1))
-            cols = slice(P * j, P * (j + 1))
-            angle = angles.tile([P, GROUP * P], F32)
-            nc.tensor.matmul_mx(
-                out=angle[:],
-                lhsT=w_codes[:, cols].bitcast(FP8X4),
-                lhsT_scale=w_plane[:, cols],
-                rhs=e_codes[:, rows, :].rearrange("p t r -> p (t r)").bitcast(FP8X4),
-                rhs_scale=e_plane[:, rows, :].rearrange("p t r -> p (t r)"),
-                start=True,
-                stop=True,
+        def e_side(first, count):
+            rows = slice(first, first + count)
+            return (
+                e_codes[:, rows, :].rearrange("p t r -> p (t r)").bitcast(FP8X4),
+                e_plane[:, rows, :].rearrange("p t r -> p (t r)"),
             )
-            angle_of[u] = angle
 
-        def whole_turns(u):
-            j = u % BLOCKS
-            whole = stage.tile([P, GROUP * P], I32)
-            nc.vector.tensor_scalar(
-                out=whole[:], in0=angle_of[u][:], scalar1=1.0 / TWO_PI, scalar2=phase[:, j : j + 1],
+        def w_side(first, count):
+            cols = slice(first, first + count)
+            return w_codes[:, cols].bitcast(FP8X4), w_plane[:, cols]
+
+        def product(key, still, moving):
+            angle = angles.tile([P, N_TILE], F32, tag="angle")
+            nc.tensor.matmul_mx(
+                out=angle[:], lhsT=still[0], lhsT_scale=still[1], rhs=moving[0], rhs_scale=moving[1],
+                start=True, stop=True,
+            )
+            angles_of[key] = angle
+
+        def row_products(t):
+            for n in range(ROW_BANKS):
+                product(("row", t, n), e_side(t, 1), w_side(N_TILE * n, N_TILE))
+
+        def row_turns(t):
+            turns = stage.tile([P, ROW_FEATURES], F32)
+            for n in range(ROW_BANKS):
+                cols = slice(N_TILE * n, N_TILE * (n + 1))
+                nc.vector.scalar_tensor_tensor(
+                    out=turns[:, cols], in0=angles_of["row", t, n][:], scalar=1.0 / TWO_PI,
+                    in1=row_phase[:, cols], op0=ALU.mult, op1=ALU.add,
+                )
+            turns_of[t] = turns
+
+        def round_turns(t):
+            shifted = rounded.tile([P, ROW_FEATURES], F32)
+            nc.scalar.activation(out=shifted[:], in_=turns_of[t][:], func=ACT.Identity, bias=magic[:])
+            shifted_of[t] = shifted
+
+        def fraction(t):
+            neg_frac = stage.tile([P, ROW_FEATURES], F32)
+            nc.vector.scalar_tensor_tensor(
+                out=neg_frac[:], in0=shifted_of[t][:], scalar=ROUND_MAGIC, in1=turns_of[t][:],
+                op0=ALU.subtract, op1=ALU.subtract,
+            )
+            part_of[t] = neg_frac
+
+        def row_pieces(t):
+            width = N_TILE if t >= TAIL_FROM else ROW_FEATURES
+            return [slice(n0, n0 + width) for n0 in range(0, ROW_FEATURES, width)]
+
+        def row_sine(t):
+            sin_row = stage.tile([P, ROW_FEATURES], F32)
+            for cols in row_pieces(t):
+                nc.scalar.activation(
+                    out=sin_row[:, cols], in_=part_of[t][:, cols], func=ACT.Sin, scale=-TWO_PI
+                )
+            sine_of[t] = sin_row
+
+        def row_factor(t):
+            if t >= TAIL_FROM:
+                for cols in row_pieces(t):
+                    nc.vector.tensor_scalar_mul(
+                        out=sine_of[t][:, cols], in0=sine_of[t][:, cols], scalar1=OUT_SCALE
+                    )
+                    nc.sync.dma_start(out=out_rows[:, t, cols], in_=sine_of[t][:, cols])
+                return
+            row_home = shifted_of[t + 2]
+            nc.gpsimd.tensor_scalar(
+                out=row_home[:], in0=sine_of[t][:], scalar1=OUT_SCALE, scalar2=0.0,
                 op0=ALU.mult, op1=ALU.add,
             )
-            whole_of[u] = whole
+            nc.sync.dma_start(out=out_rows[:, t, 0:ROW_FEATURES], in_=row_home[:])
 
-        def part_turn(u):
-            part = stage.tile([P, GROUP * P], F32)
-            nc.vector.scalar_tensor_tensor(
-                out=part[:], in0=angle_of[u][:], scalar=1.0 / TWO_PI, in1=whole_of[u][:],
-                op0=ALU.mult, op1=ALU.subtract,
-            )
-            part_of[u] = part
+        def blocks_of(s):
+            g, i = divmod(s, GROUP)
+            first = ROW_FEATURES // P + SLOT_BLOCKS * i
+            return [(g, j) for j in range(first, first + SLOT_BLOCKS)]
 
-        def sine(u):
-            j = u % BLOCKS
-            sin_u = stage.tile([P, GROUP * P], F32)
-            nc.scalar.activation(
-                out=sin_u[:], in_=part_of[u][:], func=ACT.Sin, scale=TWO_PI, bias=phase_rad[:, j : j + 1]
-            )
-            sine_of[u] = sin_u
+        def block_products(s):
+            for g, j in blocks_of(s):
+                product((g, j), w_side(P * j, P), e_side(GROUP * g, GROUP))
 
-        def turn_back(u):
-            up = upright.tile([P, GROUP, P], F32)
-            for i in range(GROUP):
-                nc.tensor.transpose(up[:, i, :], sine_of[u][:, P * i : P * (i + 1)], ident[:])
-            upright_of[u] = up
-
-        def scale_and_store(u):
-            g, j = divmod(u, BLOCKS)
-            quarter, b = divmod(j, STORE_BLOCKS)
-            if b == 0:
-                home = homes.tile([P, GROUP, QUARTER], F32)
-                home_of[g, quarter] = home
-            home = home_of[g, quarter]
-            cols = slice(P * b, P * (b + 1))
-            last = u >= UNITS - STORE_BLOCKS
-            if last and b % 2 == 0:
-                nc.vector.tensor_scalar_mul(out=home[:, :, cols], in0=upright_of[u][:], scalar1=OUT_SCALE)
-            else:
-                nc.scalar.mul(out=home[:, :, cols], in_=upright_of[u][:], mul=OUT_SCALE)
-            rows = slice(GROUP * g, GROUP * (g + 1))
-            if last:
-                nc.sync.dma_start(out=out_rows[:, rows, P * j : P * (j + 1)], in_=home[:, :, cols])
-            elif b == STORE_BLOCKS - 1:
-                nc.sync.dma_start(
-                    out=out_rows[:, rows, QUARTER * quarter : QUARTER * (quarter + 1)], in_=home[:]
+        def whole_turns(s):
+            for g, j in blocks_of(s):
+                whole = stage.tile([P, N_TILE], I32)
+                nc.vector.tensor_scalar(
+                    out=whole[:], in0=angles_of[g, j][:], scalar1=1.0 / TWO_PI, scalar2=phase[:, j : j + 1],
+                    op0=ALU.mult, op1=ALU.add,
                 )
+                whole_of[g, j] = whole
 
-        def run(stage_of, u):
-            if 0 <= u < UNITS:
-                stage_of(u)
+        def part_turns(s):
+            for g, j in blocks_of(s):
+                block_part = stage.tile([P, N_TILE], F32)
+                nc.vector.scalar_tensor_tensor(
+                    out=block_part[:], in0=angles_of[g, j][:], scalar=1.0 / TWO_PI, in1=whole_of[g, j][:],
+                    op0=ALU.mult, op1=ALU.subtract,
+                )
+                block_part_of[g, j] = block_part
+
+        def block_sines(s):
+            for g, j in blocks_of(s):
+                block_sine = stage.tile([P, N_TILE], F32)
+                nc.scalar.activation(
+                    out=block_sine[:], in_=block_part_of[g, j][:], func=ACT.Sin, scale=TWO_PI,
+                    bias=phase_rad[:, j : j + 1],
+                )
+                block_sine_of[g, j] = block_sine
+
+        def turn_back(s):
+            for g, j in blocks_of(s):
+                up = upright.tile([P, GROUP, P], F32)
+                for i in range(GROUP):
+                    nc.tensor.transpose(up[:, i, :], block_sine_of[g, j][:, P * i : P * (i + 1)], ident[:])
+                upright_of[g, j] = up
+
+        def block_factors(s):
+            for g, j in blocks_of(s):
+                part, b = divmod(j, HOME_BLOCKS)
+                if b == 0:
+                    home = homes.tile([P, GROUP, HOME_BLOCKS * P], F32)
+                    home_of[g, part] = home
+                home = home_of[g, part]
+                cols = slice(P * b, P * (b + 1))
+                nc.scalar.mul(out=home[:, :, cols], in_=upright_of[g, j][:], mul=OUT_SCALE)
+                rows = slice(GROUP * g, GROUP * (g + 1))
+                if s >= ROW_TILES - 2:
+                    nc.sync.dma_start(out=out_rows[:, rows, P * j : P * (j + 1)], in_=home[:, :, cols])
+                elif b == HOME_BLOCKS - 1:
+                    first = HOME_BLOCKS * P * part
+                    nc.sync.dma_start(out=out_rows[:, rows, first : first + HOME_BLOCKS * P], in_=home[:])
+
+        def run(stage_of, s):
+            if 0 <= s < ROW_TILES:
+                stage_of(s)
 
         with tc.manual_schedule():
             for t in (0, 1):
@@ -241,37 +322,56 @@ def tile_rff_kernel(tc, lt_weight, Lambdas_words, Lambdas_scales, bias, out):
                 out=phase_rad[:], in0=bias_columns[:, 0:BLOCKS], scalar1=1.0, scalar2=0.5 * math.pi,
                 op0=ALU.mult, op1=ALU.add,
             )
+            for n0 in range(0, ROW_FEATURES, N_TILE):
+                spread = upright.tile([P, N_TILE], F32, tag="up")
+                nc.tensor.matmul(
+                    out=spread[:], lhsT=ones[:], rhs=bias_row[:, n0 : n0 + N_TILE], start=True, stop=True
+                )
+                nc.vector.tensor_scalar(
+                    out=row_phase[:, n0 : n0 + N_TILE], in0=spread[:], scalar1=1.0 / TWO_PI, scalar2=0.25,
+                    op0=ALU.mult, op1=ALU.add,
+                )
             for t in range(GROUP):
                 clip_rows(t, nc.vector)
-                flip(t)
+            for t in range(GROUP):
+                flip(t, angles, "angle")
             for t in range(GROUP):
                 regroup(t, nc.vector.tensor_copy if t % 2 == 0 else nc.scalar.copy)
             for t in range(GROUP):
                 quantise(t)
+            for t in (8, 9):
+                sum_squares_on_scalar(t)
             clip_factors(1)
+            for t in (10, 11):
+                sum_squares_on_scalar(t)
 
-            for k in range(-5, UNITS + 4):
-                run(multiply, k + 2)
-                run(turn_back, k - 3)
-                for t in range(GROUP, ROW_TILES):
-                    g, i = divmod(t, GROUP)
-                    begin = BLOCKS * (g - 1) + 4 * i - 5
-                    if g >= 2 and k == BLOCKS * (g - 2) + 2 * i + 1:
-                        if i % 2 == 0:
-                            sum_squares_on_scalar(t)
-                        else:
-                            sum_squares_on_vector(t)
-                    if g >= 2 and i == 0 and k == begin - 2:
-                        clip_factors(g)
-                    if k == begin:
-                        clip_rows(t, nc.gpsimd)
-                    if k == begin + 1:
-                        flip(t)
-                    if k == begin + 2:
-                        regroup(t, nc.scalar.copy)
-                    if k == begin + 3:
-                        quantise(t)
+            for k in range(-3, ROW_TILES + 4):
+                if k == 0:
+                    clip_factors(2)
+                if k in (4, 8, 12):
+                    clip_factors(k // GROUP + 2)
+                run(row_products, k + 1)
+                run(block_factors, k - 2)
+                run(block_sines, k - 1)
+                run(turn_back, k - 1)
+                if GROUP <= k + 6 < ROW_TILES:
+                    flip(k + 6, flipped, "flip")
+                run(block_products, k + 1)
+                run(row_turns, k)
                 run(whole_turns, k)
-                run(part_turn, k - 1)
-                run(sine, k - 2)
-                run(scale_and_store, k - 4)
+                run(part_turns, k)
+                if GROUP <= k + 5 < ROW_TILES:
+                    regroup(k + 5, nc.scalar.copy)
+                run(row_sine, k - 2)
+                run(round_turns, k)
+                if 0 <= k < ROW_TILES - 12:
+                    if k % 2 == 0:
+                        sum_squares_on_scalar(k + 12)
+                    else:
+                        sum_squares_on_vector(k + 12)
+                if GROUP <= k + 5 < ROW_TILES:
+                    quantise(k + 5)
+                run(fraction, k - 1)
+                run(row_factor, k - 3)
+                if GROUP <= k + 7 < ROW_TILES:
+                    clip_rows(k + 7, nc.gpsimd)

@@ -26,6 +26,7 @@ ROW_FEATURES = ROW_BANKS * N_TILE
 BLOCKS = FDIM // P
 SLOT_BLOCKS = (BLOCKS - ROW_FEATURES // P) // GROUP
 HOME_BLOCKS = 4
+GPSIMD_ROUNDS_FROM = N_TILE
 TAIL_FROM = ROW_TILES - 2
 EPS = 1e-5
 MAX_NORM = 1.0 - EPS
@@ -202,10 +203,19 @@ def tile_rff_kernel(tc, lt_weight, Lambdas_words, Lambdas_scales, bias, out):
                 )
             turns_of[t] = turns
 
-        def round_turns(t):
+        def round_on_scalar(t):
             shifted = rounded.tile([P, ROW_FEATURES], F32)
-            nc.scalar.activation(out=shifted[:], in_=turns_of[t][:], func=ACT.Identity, bias=magic[:])
+            nc.scalar.activation(
+                out=shifted[:, :GPSIMD_ROUNDS_FROM], in_=turns_of[t][:, :GPSIMD_ROUNDS_FROM],
+                func=ACT.Identity, bias=magic[:],
+            )
             shifted_of[t] = shifted
+
+        def round_on_gpsimd(t):
+            nc.gpsimd.tensor_scalar(
+                out=shifted_of[t][:, GPSIMD_ROUNDS_FROM:], in0=turns_of[t][:, GPSIMD_ROUNDS_FROM:],
+                scalar1=1.0, scalar2=ROUND_MAGIC, op0=ALU.mult, op1=ALU.add,
+            )
 
         def fraction(t):
             neg_frac = stage.tile([P, ROW_FEATURES], F32)
@@ -293,9 +303,12 @@ def tile_rff_kernel(tc, lt_weight, Lambdas_words, Lambdas_scales, bias, out):
                     home_of[g, part] = home
                 home = home_of[g, part]
                 cols = slice(P * b, P * (b + 1))
-                nc.scalar.mul(out=home[:, :, cols], in_=upright_of[g, j][:], mul=OUT_SCALE)
+                if s >= TAIL_FROM:
+                    nc.vector.tensor_scalar_mul(out=home[:, :, cols], in0=upright_of[g, j][:], scalar1=OUT_SCALE)
+                else:
+                    nc.scalar.mul(out=home[:, :, cols], in_=upright_of[g, j][:], mul=OUT_SCALE)
                 rows = slice(GROUP * g, GROUP * (g + 1))
-                if s >= ROW_TILES - 2:
+                if s >= TAIL_FROM:
                     nc.sync.dma_start(out=out_rows[:, rows, P * j : P * (j + 1)], in_=home[:, :, cols])
                 elif b == HOME_BLOCKS - 1:
                     first = HOME_BLOCKS * P * part
@@ -306,9 +319,9 @@ def tile_rff_kernel(tc, lt_weight, Lambdas_words, Lambdas_scales, bias, out):
                 stage_of(s)
 
         with tc.manual_schedule():
-            for t in (0, 1):
+            for t in (0, 1, 4, 5):
                 sum_squares_on_vector(t)
-            for t in (2, 3, 4, 5, 6, 7):
+            for t in (2, 3, 6, 7, 8, 9, 10, 11):
                 sum_squares_on_scalar(t)
             clip_factors(0)
 
@@ -339,39 +352,31 @@ def tile_rff_kernel(tc, lt_weight, Lambdas_words, Lambdas_scales, bias, out):
                 regroup(t, nc.vector.tensor_copy if t % 2 == 0 else nc.scalar.copy)
             for t in range(GROUP):
                 quantise(t)
-            for t in (8, 9):
-                sum_squares_on_scalar(t)
             clip_factors(1)
-            for t in (10, 11):
-                sum_squares_on_scalar(t)
 
-            for k in range(-3, ROW_TILES + 4):
-                if k == 0:
-                    clip_factors(2)
-                if k in (4, 8, 12):
+            for k in range(-2, ROW_TILES + 4):
+                if 1 <= k and k % GROUP == 1 and k // GROUP + 2 < GROUPS:
                     clip_factors(k // GROUP + 2)
                 run(row_products, k + 1)
                 run(block_factors, k - 2)
                 run(block_sines, k - 1)
                 run(turn_back, k - 1)
-                if GROUP <= k + 6 < ROW_TILES:
-                    flip(k + 6, flipped, "flip")
-                run(block_products, k + 1)
+                if GROUP <= k + 5 < ROW_TILES:
+                    flip(k + 5, flipped, "flip")
                 run(row_turns, k)
                 run(whole_turns, k)
                 run(part_turns, k)
-                if GROUP <= k + 5 < ROW_TILES:
-                    regroup(k + 5, nc.scalar.copy)
+                if GROUP <= k + 4 < ROW_TILES:
+                    regroup(k + 4, nc.scalar.copy)
                 run(row_sine, k - 2)
-                run(round_turns, k)
+                run(round_on_scalar, k)
                 if 0 <= k < ROW_TILES - 12:
-                    if k % 2 == 0:
-                        sum_squares_on_scalar(k + 12)
-                    else:
-                        sum_squares_on_vector(k + 12)
-                if GROUP <= k + 5 < ROW_TILES:
-                    quantise(k + 5)
+                    sum_squares_on_scalar(k + 12)
+                if GROUP <= k + 4 < ROW_TILES:
+                    quantise(k + 4)
+                run(block_products, k + 1)
                 run(fraction, k - 1)
                 run(row_factor, k - 3)
-                if GROUP <= k + 7 < ROW_TILES:
-                    clip_rows(k + 7, nc.gpsimd)
+                run(round_on_gpsimd, k)
+                if GROUP <= k + 6 < ROW_TILES:
+                    clip_rows(k + 6, nc.gpsimd)

@@ -27,7 +27,7 @@ BLOCKS = FDIM // P
 SLOT_BLOCKS = (BLOCKS - ROW_FEATURES // P) // GROUP
 HOME_BLOCKS = 4
 GPSIMD_ROUNDS_FROM = N_TILE
-TAIL_FROM = ROW_TILES - 2
+LAST = ROW_TILES - 1
 EPS = 1e-5
 MAX_NORM = 1.0 - EPS
 TWO_PI = 2.0 * math.pi
@@ -102,7 +102,7 @@ def tile_rff_kernel(tc, lt_weight, Lambdas_words, Lambdas_scales, bias, out):
         for g in range(3, GROUPS):
             load_group(g)
 
-        e_of = {}
+        words_of = {}
         flipped_of = {}
         grouped_of = {}
         angles_of = {}
@@ -143,19 +143,26 @@ def tile_rff_kernel(tc, lt_weight, Lambdas_words, Lambdas_scales, bias, out):
                 op0=ALU.mult, op1=ALU.min,
             )
 
-        def clip_rows(t, engine):
+        def clip_rows(t):
             e_sb = stage.tile([P, DIM], BF16)
-            engine.tensor_scalar(
-                out=e_sb[:], in0=x_sb[:, t, :], scalar1=clip[:, t : t + 1], scalar2=0.0,
-                op0=ALU.mult, op1=ALU.add,
+            nc.vector.tensor_scalar_mul(out=e_sb[:], in0=x_sb[:, t, :], scalar1=clip[:, t : t + 1])
+            e_words = e_sb[:].bitcast(F32)
+            words_of[t] = [e_words[:, u : DIM // 2 : HALVES] for u in range(HALVES)]
+
+        def clip_and_sort_rows(t):
+            e_sorted = stage.tile([P, DIM], BF16)
+            nc.gpsimd.tensor_scalar(
+                out=e_sorted[:].rearrange("p (u w e) -> p u w e", u=HALVES, w=P),
+                in0=x_sb[:, t, :].rearrange("p (w u e) -> p u w e", u=HALVES, w=P),
+                scalar1=clip[:, t : t + 1], scalar2=0.0, op0=ALU.mult, op1=ALU.add,
             )
-            e_of[t] = e_sb
+            e_words = e_sorted[:].bitcast(F32)
+            words_of[t] = [e_words[:, P * u : P * (u + 1)] for u in range(HALVES)]
 
         def flip(t, pool, tag):
-            e_words = e_of[t][:].bitcast(F32)
             e_t = pool.tile([P, HALVES, P], F32, tag=tag)
             for u in range(HALVES):
-                nc.tensor.transpose(e_t[:, u, :], e_words[:, u : DIM // 2 : HALVES], ident[:])
+                nc.tensor.transpose(e_t[:, u, :], words_of[t][u], ident[:])
             flipped_of[t] = e_t
 
         def regroup(t, copy_words):
@@ -204,10 +211,10 @@ def tile_rff_kernel(tc, lt_weight, Lambdas_words, Lambdas_scales, bias, out):
             turns_of[t] = turns
 
         def round_on_scalar(t):
+            cols = slice(0, ROW_FEATURES if t == LAST else GPSIMD_ROUNDS_FROM)
             shifted = rounded.tile([P, ROW_FEATURES], F32)
             nc.scalar.activation(
-                out=shifted[:, :GPSIMD_ROUNDS_FROM], in_=turns_of[t][:, :GPSIMD_ROUNDS_FROM],
-                func=ACT.Identity, bias=magic[:],
+                out=shifted[:, cols], in_=turns_of[t][:, cols], func=ACT.Identity, bias=magic[:]
             )
             shifted_of[t] = shifted
 
@@ -226,7 +233,7 @@ def tile_rff_kernel(tc, lt_weight, Lambdas_words, Lambdas_scales, bias, out):
             part_of[t] = neg_frac
 
         def row_pieces(t):
-            width = N_TILE if t >= TAIL_FROM else ROW_FEATURES
+            width = N_TILE if t == LAST else ROW_FEATURES
             return [slice(n0, n0 + width) for n0 in range(0, ROW_FEATURES, width)]
 
         def row_sine(t):
@@ -238,14 +245,14 @@ def tile_rff_kernel(tc, lt_weight, Lambdas_words, Lambdas_scales, bias, out):
             sine_of[t] = sin_row
 
         def row_factor(t):
-            if t >= TAIL_FROM:
+            if t == LAST:
                 for cols in row_pieces(t):
                     nc.vector.tensor_scalar_mul(
                         out=sine_of[t][:, cols], in0=sine_of[t][:, cols], scalar1=OUT_SCALE
                     )
                     nc.sync.dma_start(out=out_rows[:, t, cols], in_=sine_of[t][:, cols])
                 return
-            row_home = shifted_of[t + 2]
+            row_home = shifted_of[t + 2] if t + 2 <= LAST else sine_of[t]
             nc.gpsimd.tensor_scalar(
                 out=row_home[:], in0=sine_of[t][:], scalar1=OUT_SCALE, scalar2=0.0,
                 op0=ALU.mult, op1=ALU.add,
@@ -303,12 +310,12 @@ def tile_rff_kernel(tc, lt_weight, Lambdas_words, Lambdas_scales, bias, out):
                     home_of[g, part] = home
                 home = home_of[g, part]
                 cols = slice(P * b, P * (b + 1))
-                if s >= TAIL_FROM:
+                if s == LAST:
                     nc.vector.tensor_scalar_mul(out=home[:, :, cols], in0=upright_of[g, j][:], scalar1=OUT_SCALE)
                 else:
                     nc.scalar.mul(out=home[:, :, cols], in_=upright_of[g, j][:], mul=OUT_SCALE)
                 rows = slice(GROUP * g, GROUP * (g + 1))
-                if s >= TAIL_FROM:
+                if s >= LAST - 1:
                     nc.sync.dma_start(out=out_rows[:, rows, P * j : P * (j + 1)], in_=home[:, :, cols])
                 elif b == HOME_BLOCKS - 1:
                     first = HOME_BLOCKS * P * part
@@ -335,26 +342,36 @@ def tile_rff_kernel(tc, lt_weight, Lambdas_words, Lambdas_scales, bias, out):
                 out=phase_rad[:], in0=bias_columns[:, 0:BLOCKS], scalar1=1.0, scalar2=0.5 * math.pi,
                 op0=ALU.mult, op1=ALU.add,
             )
+            spreads = []
             for n0 in range(0, ROW_FEATURES, N_TILE):
                 spread = upright.tile([P, N_TILE], F32, tag="up")
                 nc.tensor.matmul(
                     out=spread[:], lhsT=ones[:], rhs=bias_row[:, n0 : n0 + N_TILE], start=True, stop=True
                 )
+                spreads.append(spread)
+
+            def spread_to_phase(n):
                 nc.vector.tensor_scalar(
-                    out=row_phase[:, n0 : n0 + N_TILE], in0=spread[:], scalar1=1.0 / TWO_PI, scalar2=0.25,
-                    op0=ALU.mult, op1=ALU.add,
+                    out=row_phase[:, N_TILE * n : N_TILE * (n + 1)], in0=spreads[n][:],
+                    scalar1=1.0 / TWO_PI, scalar2=0.25, op0=ALU.mult, op1=ALU.add,
                 )
+
+            spread_to_phase(0)
             for t in range(GROUP):
-                clip_rows(t, nc.vector)
+                clip_rows(t)
+            spread_to_phase(1)
             for t in range(GROUP):
                 flip(t, angles, "angle")
-            for t in range(GROUP):
-                regroup(t, nc.vector.tensor_copy if t % 2 == 0 else nc.scalar.copy)
-            for t in range(GROUP):
+            regroup(0, nc.vector.tensor_copy)
+            quantise(0)
+            regroup(1, nc.scalar.copy)
+            regroup(3, nc.scalar.copy)
+            regroup(2, nc.vector.tensor_copy)
+            for t in (1, 2, 3):
                 quantise(t)
             clip_factors(1)
 
-            for k in range(-2, ROW_TILES + 4):
+            for k in range(-2, ROW_TILES):
                 if 1 <= k and k % GROUP == 1 and k // GROUP + 2 < GROUPS:
                     clip_factors(k // GROUP + 2)
                 run(row_products, k + 1)
@@ -377,6 +394,17 @@ def tile_rff_kernel(tc, lt_weight, Lambdas_words, Lambdas_scales, bias, out):
                 run(block_products, k + 1)
                 run(fraction, k - 1)
                 run(row_factor, k - 3)
-                run(round_on_gpsimd, k)
+                if 0 <= k < LAST:
+                    round_on_gpsimd(k)
                 if GROUP <= k + 6 < ROW_TILES:
-                    clip_rows(k + 6, nc.gpsimd)
+                    clip_and_sort_rows(k + 6)
+            fraction(LAST)
+            block_sines(LAST)
+            turn_back(LAST)
+            block_factors(LAST - 1)
+            row_sine(LAST - 1)
+            row_sine(LAST)
+            row_factor(LAST - 2)
+            row_factor(LAST - 1)
+            block_factors(LAST)
+            row_factor(LAST)

@@ -90,19 +90,24 @@ def tile_rff_kernel(tc, lt_weight, Lambdas_words, Lambdas_scales, bias, out):
                 out=x_sb[:, GROUP * g : GROUP * (g + 1), :], in_=x_rows[:, GROUP * g : GROUP * (g + 1), :]
             )
 
-        for g in range(3):
-            load_group(g)
+        load_group(0)
         for q in range(4):
             nc.sync.dma_start(
                 out=w_plane[32 * q : 32 * q + 4, :].bitcast(I32),
                 in_=Lambdas_scales[0, 4 * q : 4 * q + 4, :].bitcast(I32),
             )
-        for n0 in range(0, FDIM, N_TILE):
-            nc.sync.dma_start(out=w_codes[:, n0 : n0 + N_TILE].bitcast(I32), in_=w_hbm[:, n0 : n0 + N_TILE])
-        for g in range(3, GROUPS):
+
+        def load_weight(first, count):
+            cols = slice(first, first + count)
+            nc.sync.dma_start(out=w_codes[:, cols].bitcast(I32), in_=w_hbm[:, cols])
+
+        load_weight(0, ROW_FEATURES)
+        load_group(1)
+        load_weight(ROW_FEATURES, FDIM - ROW_FEATURES)
+        for g in range(2, GROUPS):
             load_group(g)
 
-        words_of = {}
+        e_of = {}
         flipped_of = {}
         grouped_of = {}
         angles_of = {}
@@ -146,23 +151,21 @@ def tile_rff_kernel(tc, lt_weight, Lambdas_words, Lambdas_scales, bias, out):
         def clip_rows(t):
             e_sb = stage.tile([P, DIM], BF16)
             nc.vector.tensor_scalar_mul(out=e_sb[:], in0=x_sb[:, t, :], scalar1=clip[:, t : t + 1])
-            e_words = e_sb[:].bitcast(F32)
-            words_of[t] = [e_words[:, u : DIM // 2 : HALVES] for u in range(HALVES)]
+            e_of[t] = e_sb
 
-        def clip_and_sort_rows(t):
-            e_sorted = stage.tile([P, DIM], BF16)
+        def clip_rows_on_gpsimd(t):
+            e_sb = stage.tile([P, DIM], BF16)
             nc.gpsimd.tensor_scalar(
-                out=e_sorted[:].rearrange("p (u w e) -> p u w e", u=HALVES, w=P),
-                in0=x_sb[:, t, :].rearrange("p (w u e) -> p u w e", u=HALVES, w=P),
-                scalar1=clip[:, t : t + 1], scalar2=0.0, op0=ALU.mult, op1=ALU.add,
+                out=e_sb[:], in0=x_sb[:, t, :], scalar1=clip[:, t : t + 1], scalar2=0.0,
+                op0=ALU.mult, op1=ALU.add,
             )
-            e_words = e_sorted[:].bitcast(F32)
-            words_of[t] = [e_words[:, P * u : P * (u + 1)] for u in range(HALVES)]
+            e_of[t] = e_sb
 
         def flip(t, pool, tag):
+            e_words = e_of[t][:].bitcast(F32)
             e_t = pool.tile([P, HALVES, P], F32, tag=tag)
             for u in range(HALVES):
-                nc.tensor.transpose(e_t[:, u, :], words_of[t][u], ident[:])
+                nc.tensor.transpose(e_t[:, u, :], e_words[:, u : DIM // 2 : HALVES], ident[:])
             flipped_of[t] = e_t
 
         def regroup(t, copy_words):
@@ -326,9 +329,9 @@ def tile_rff_kernel(tc, lt_weight, Lambdas_words, Lambdas_scales, bias, out):
                 stage_of(s)
 
         with tc.manual_schedule():
-            for t in (0, 1, 4, 5):
+            for t in (0, 1):
                 sum_squares_on_vector(t)
-            for t in (2, 3, 6, 7, 8, 9, 10, 11):
+            for t in (2, 3, 4, 5, 6, 7):
                 sum_squares_on_scalar(t)
             clip_factors(0)
 
@@ -366,6 +369,8 @@ def tile_rff_kernel(tc, lt_weight, Lambdas_words, Lambdas_scales, bias, out):
             quantise(0)
             regroup(1, nc.scalar.copy)
             regroup(3, nc.scalar.copy)
+            for t in (8, 9, 10, 11):
+                sum_squares_on_scalar(t)
             regroup(2, nc.vector.tensor_copy)
             for t in (1, 2, 3):
                 quantise(t)
@@ -378,7 +383,7 @@ def tile_rff_kernel(tc, lt_weight, Lambdas_words, Lambdas_scales, bias, out):
                 run(block_factors, k - 2)
                 run(block_sines, k - 1)
                 run(turn_back, k - 1)
-                if GROUP <= k + 5 < ROW_TILES:
+                if k >= 0 and k + 5 < ROW_TILES:
                     flip(k + 5, flipped, "flip")
                 run(row_turns, k)
                 run(whole_turns, k)
@@ -392,12 +397,14 @@ def tile_rff_kernel(tc, lt_weight, Lambdas_words, Lambdas_scales, bias, out):
                 if GROUP <= k + 4 < ROW_TILES:
                     quantise(k + 4)
                 run(block_products, k + 1)
+                if k == -1:
+                    flip(GROUP, flipped, "flip")
                 run(fraction, k - 1)
                 run(row_factor, k - 3)
                 if 0 <= k < LAST:
                     round_on_gpsimd(k)
                 if GROUP <= k + 6 < ROW_TILES:
-                    clip_and_sort_rows(k + 6)
+                    clip_rows_on_gpsimd(k + 6)
             fraction(LAST)
             block_sines(LAST)
             turn_back(LAST)

@@ -153,14 +153,6 @@ def tile_rff_kernel(tc, lt_weight, Lambdas_words, Lambdas_scales, bias, out):
             nc.vector.tensor_scalar_mul(out=e_sb[:], in0=x_sb[:, t, :], scalar1=clip[:, t : t + 1])
             e_of[t] = e_sb
 
-        def clip_rows_on_gpsimd(t):
-            e_sb = stage.tile([P, DIM], BF16)
-            nc.gpsimd.tensor_scalar(
-                out=e_sb[:], in0=x_sb[:, t, :], scalar1=clip[:, t : t + 1], scalar2=0.0,
-                op0=ALU.mult, op1=ALU.add,
-            )
-            e_of[t] = e_sb
-
         def flip(t, pool, tag):
             e_words = e_of[t][:].bitcast(F32)
             e_t = pool.tile([P, HALVES, P], F32, tag=tag)
@@ -396,6 +388,8 @@ def tile_rff_kernel(tc, lt_weight, Lambdas_words, Lambdas_scales, bias, out):
                     sum_squares_on_scalar(k + 12)
                 if GROUP <= k + 4 < ROW_TILES:
                     quantise(k + 4)
+                if GROUP <= k + 6 < ROW_TILES:
+                    clip_rows(k + 6)
                 run(block_products, k + 1)
                 if k == -1:
                     flip(GROUP, flipped, "flip")
@@ -403,8 +397,7 @@ def tile_rff_kernel(tc, lt_weight, Lambdas_words, Lambdas_scales, bias, out):
                 run(row_factor, k - 3)
                 if 0 <= k < LAST:
                     round_on_gpsimd(k)
-                if GROUP <= k + 6 < ROW_TILES:
-                    clip_rows_on_gpsimd(k + 6)
+
             fraction(LAST)
             block_sines(LAST)
             turn_back(LAST)

@@ -27,6 +27,7 @@ BLOCKS = FDIM // P
 SLOT_BLOCKS = (BLOCKS - ROW_FEATURES // P) // GROUP
 HOME_BLOCKS = 4
 GPSIMD_ROUNDS_FROM = N_TILE
+SCALAR_CLIPS_FROM = 18
 LAST = ROW_TILES - 1
 EPS = 1e-5
 MAX_NORM = 1.0 - EPS
@@ -150,8 +151,14 @@ def tile_rff_kernel(tc, lt_weight, Lambdas_words, Lambdas_scales, bias, out):
 
         def clip_rows(t):
             e_sb = stage.tile([P, DIM], BF16)
-            nc.vector.tensor_scalar_mul(out=e_sb[:], in0=x_sb[:, t, :], scalar1=clip[:, t : t + 1])
+            if clips_on_scalar(t):
+                nc.scalar.activation(out=e_sb[:], in_=x_sb[:, t, :], func=ACT.Copy, scale=clip[:, t : t + 1])
+            else:
+                nc.vector.tensor_scalar_mul(out=e_sb[:], in0=x_sb[:, t, :], scalar1=clip[:, t : t + 1])
             e_of[t] = e_sb
+
+        def clips_on_scalar(t):
+            return t in (GROUP, GROUP + 1) or t >= SCALAR_CLIPS_FROM
 
         def flip(t, pool, tag):
             e_words = e_of[t][:].bitcast(F32)
@@ -228,7 +235,7 @@ def tile_rff_kernel(tc, lt_weight, Lambdas_words, Lambdas_scales, bias, out):
             part_of[t] = neg_frac
 
         def row_pieces(t):
-            width = N_TILE if t == LAST else ROW_FEATURES
+            width = N_TILE if t >= LAST - 1 else ROW_FEATURES
             return [slice(n0, n0 + width) for n0 in range(0, ROW_FEATURES, width)]
 
         def row_sine(t):
@@ -240,19 +247,18 @@ def tile_rff_kernel(tc, lt_weight, Lambdas_words, Lambdas_scales, bias, out):
             sine_of[t] = sin_row
 
         def row_factor(t):
-            if t == LAST:
-                for cols in row_pieces(t):
+            row_home = shifted_of[t + 2] if t < LAST - 3 else sine_of[t]
+            for cols in row_pieces(t):
+                if t == LAST:
                     nc.vector.tensor_scalar_mul(
-                        out=sine_of[t][:, cols], in0=sine_of[t][:, cols], scalar1=OUT_SCALE
+                        out=row_home[:, cols], in0=sine_of[t][:, cols], scalar1=OUT_SCALE
                     )
-                    nc.sync.dma_start(out=out_rows[:, t, cols], in_=sine_of[t][:, cols])
-                return
-            row_home = shifted_of[t + 2] if t + 2 <= LAST else sine_of[t]
-            nc.gpsimd.tensor_scalar(
-                out=row_home[:], in0=sine_of[t][:], scalar1=OUT_SCALE, scalar2=0.0,
-                op0=ALU.mult, op1=ALU.add,
-            )
-            nc.sync.dma_start(out=out_rows[:, t, 0:ROW_FEATURES], in_=row_home[:])
+                else:
+                    nc.gpsimd.tensor_scalar(
+                        out=row_home[:, cols], in0=sine_of[t][:, cols], scalar1=OUT_SCALE, scalar2=0.0,
+                        op0=ALU.mult, op1=ALU.add,
+                    )
+                nc.sync.dma_start(out=out_rows[:, t, cols], in_=row_home[:, cols])
 
         def blocks_of(s):
             g, i = divmod(s, GROUP)
@@ -292,7 +298,8 @@ def tile_rff_kernel(tc, lt_weight, Lambdas_words, Lambdas_scales, bias, out):
 
         def turn_back(s):
             for g, j in blocks_of(s):
-                up = upright.tile([P, GROUP, P], F32)
+                pool, tag = (angles, "angle") if s == LAST else (upright, "up")
+                up = pool.tile([P, GROUP, P], F32, tag=tag)
                 for i in range(GROUP):
                     nc.tensor.transpose(up[:, i, :], block_sine_of[g, j][:, P * i : P * (i + 1)], ident[:])
                 upright_of[g, j] = up
@@ -305,7 +312,7 @@ def tile_rff_kernel(tc, lt_weight, Lambdas_words, Lambdas_scales, bias, out):
                     home_of[g, part] = home
                 home = home_of[g, part]
                 cols = slice(P * b, P * (b + 1))
-                if s == LAST:
+                if s == LAST - 1 or (s == LAST and b % 2 == 0):
                     nc.vector.tensor_scalar_mul(out=home[:, :, cols], in0=upright_of[g, j][:], scalar1=OUT_SCALE)
                 else:
                     nc.scalar.mul(out=home[:, :, cols], in_=upright_of[g, j][:], mul=OUT_SCALE)
@@ -361,12 +368,16 @@ def tile_rff_kernel(tc, lt_weight, Lambdas_words, Lambdas_scales, bias, out):
             quantise(0)
             regroup(1, nc.scalar.copy)
             regroup(3, nc.scalar.copy)
-            for t in (8, 9, 10, 11):
-                sum_squares_on_scalar(t)
             regroup(2, nc.vector.tensor_copy)
             for t in (1, 2, 3):
                 quantise(t)
             clip_factors(1)
+            for t in (8, 9):
+                sum_squares_on_scalar(t)
+            clip_rows(4)
+            for t in (10, 11):
+                sum_squares_on_scalar(t)
+            clip_rows(5)
 
             for k in range(-2, ROW_TILES):
                 if 1 <= k and k % GROUP == 1 and k // GROUP + 2 < GROUPS:
@@ -386,9 +397,11 @@ def tile_rff_kernel(tc, lt_weight, Lambdas_words, Lambdas_scales, bias, out):
                 run(round_on_scalar, k)
                 if 0 <= k < ROW_TILES - 12:
                     sum_squares_on_scalar(k + 12)
+                if 0 <= k and k + 6 < ROW_TILES and clips_on_scalar(k + 6):
+                    clip_rows(k + 6)
                 if GROUP <= k + 4 < ROW_TILES:
                     quantise(k + 4)
-                if GROUP <= k + 6 < ROW_TILES:
+                if 0 <= k and k + 6 < ROW_TILES and not clips_on_scalar(k + 6):
                     clip_rows(k + 6)
                 run(block_products, k + 1)
                 if k == -1:
@@ -398,13 +411,13 @@ def tile_rff_kernel(tc, lt_weight, Lambdas_words, Lambdas_scales, bias, out):
                 if 0 <= k < LAST:
                     round_on_gpsimd(k)
 
+            row_factor(LAST - 2)
             fraction(LAST)
             block_sines(LAST)
             turn_back(LAST)
-            block_factors(LAST - 1)
             row_sine(LAST - 1)
-            row_sine(LAST)
-            row_factor(LAST - 2)
             row_factor(LAST - 1)
+            block_factors(LAST - 1)
+            row_sine(LAST)
             block_factors(LAST)
             row_factor(LAST)

@@ -14,12 +14,14 @@ ACT = mybir.ActivationFunctionType
 ALU = mybir.AluOpType
 
 P = 128
+PAIR = 2
 PACK = 4
 HALVES = 2
 SIZE, DIM, FDIM = 3072, 512, 2048
 ROW_TILES = SIZE // P
 GROUP = 4
 GROUPS = ROW_TILES // GROUP
+GROUP_PAD = 8
 N_TILE = 512
 ROW_BANKS = 2
 ROW_FEATURES = ROW_BANKS * N_TILE
@@ -67,9 +69,9 @@ def tile_rff_kernel(tc, lt_weight, Lambdas_words, Lambdas_scales, bias, out):
         magic = keep.tile([P, 1], F32)
         warm = keep.tile([P, 1], F32)
         sumsq = keep.tile([P, ROW_TILES], F32)
-        floored = keep.tile([P, ROW_TILES], F32)
-        inv_norm = keep.tile([P, ROW_TILES], F32)
-        clip = keep.tile([P, ROW_TILES], F32)
+        floored = keep.tile([P, GROUPS, GROUP_PAD], F32)
+        inv_norm = keep.tile([P, GROUPS, GROUP_PAD], F32)
+        clip = keep.tile([P, GROUPS, GROUP_PAD], F32)
         e_codes = keep.tile([P, ROW_TILES, P], U32, align_bytes=64)
         e_plane = keep.tile([P, ROW_TILES, P], U8, align_bytes=64)
 
@@ -135,26 +137,36 @@ def tile_rff_kernel(tc, lt_weight, Lambdas_words, Lambdas_scales, bias, out):
                 op0=ALU.mult, op1=ALU.mult, accum_out=sumsq[:, t : t + 1],
             )
 
-        def clip_factors(g):
-            some = slice(GROUP * g, GROUP * (g + 1))
-            nc.gpsimd.tensor_scalar(
-                out=floored[:, some], in0=sumsq[:, some], scalar1=EPS * EPS, scalar2=0.0,
-                op0=ALU.max, op1=ALU.add,
+        def floor_norms(g, engine):
+            engine.tensor_scalar(
+                out=floored[:, g, 0:GROUP], in0=sumsq[:, GROUP * g : GROUP * (g + 1)], scalar1=EPS * EPS,
+                scalar2=0.0, op0=ALU.max, op1=ALU.add,
             )
+
+        def inverse_norms(g):
             nc.gpsimd.tensor_tensor(
-                out=inv_norm[:, some], in0=floored[:, some], in1=minus_half[:], op=ALU.pow
+                out=inv_norm[:, g, 0:GROUP], in0=floored[:, g, 0:GROUP], in1=minus_half[:], op=ALU.pow
             )
-            nc.gpsimd.tensor_scalar(
-                out=clip[:, some], in0=inv_norm[:, some], scalar1=MAX_NORM, scalar2=1.0,
+
+        def clip_factors(g, engine):
+            engine.tensor_scalar(
+                out=clip[:, g, 0:GROUP], in0=inv_norm[:, g, 0:GROUP], scalar1=MAX_NORM, scalar2=1.0,
                 op0=ALU.mult, op1=ALU.min,
             )
 
+        def all_clip_factors(g):
+            floor_norms(g, nc.gpsimd)
+            inverse_norms(g)
+            clip_factors(g, nc.gpsimd)
+
         def clip_rows(t):
+            g, i = divmod(t, GROUP)
+            factor = clip[:, g, i : i + 1]
             e_sb = stage.tile([P, DIM], BF16)
             if clips_on_scalar(t):
-                nc.scalar.activation(out=e_sb[:], in_=x_sb[:, t, :], func=ACT.Copy, scale=clip[:, t : t + 1])
+                nc.scalar.activation(out=e_sb[:], in_=x_sb[:, t, :], func=ACT.Copy, scale=factor)
             else:
-                nc.vector.tensor_scalar_mul(out=e_sb[:], in0=x_sb[:, t, :], scalar1=clip[:, t : t + 1])
+                nc.vector.tensor_scalar_mul(out=e_sb[:], in0=x_sb[:, t, :], scalar1=factor)
             e_of[t] = e_sb
 
         def clips_on_scalar(t):
@@ -168,15 +180,19 @@ def tile_rff_kernel(tc, lt_weight, Lambdas_words, Lambdas_scales, bias, out):
             flipped_of[t] = e_t
 
         def regroup(t, copy_words):
-            grouped = stage.tile([P, P, PACK], BF16, align_bytes=64)
-            copy_words(out=grouped[:].bitcast(F32), in_=flipped_of[t][:].rearrange("p u r -> p r u"))
-            grouped_of[t] = grouped
+            if t % PAIR == 0:
+                grouped = stage.tile([P, PAIR, P * PACK], BF16, align_bytes=64)
+                grouped_of[t // PAIR] = grouped
+            copy_words(
+                out=grouped_of[t // PAIR][:, t % PAIR, :].bitcast(F32),
+                in_=flipped_of[t][:].rearrange("p u r -> p r u"),
+            )
 
-        def quantise(t):
+        def quantise(t, count):
+            some = slice(t % PAIR, t % PAIR + count)
+            codes, plane = e_side(t, count)
             nc.vector.quantize_mx(
-                out=e_codes[:, t, :].bitcast(FP8X4),
-                scales=e_plane[:, t, :],
-                in_=grouped_of[t][:].rearrange("p r t -> p (r t)"),
+                out=codes, scales=plane, in_=grouped_of[t // PAIR][:, some, :].rearrange("p t r -> p (t r)")
             )
 
         def e_side(first, count):
@@ -272,9 +288,9 @@ def tile_rff_kernel(tc, lt_weight, Lambdas_words, Lambdas_scales, bias, out):
         def whole_turns(s):
             for g, j in blocks_of(s):
                 whole = stage.tile([P, N_TILE], I32)
-                nc.vector.tensor_scalar(
-                    out=whole[:], in0=angles_of[g, j][:], scalar1=1.0 / TWO_PI, scalar2=phase[:, j : j + 1],
-                    op0=ALU.mult, op1=ALU.add,
+                nc.vector.scalar_tensor_tensor(
+                    out=whole[:], in0=angles_of[g, j][:], scalar=1.0 / TWO_PI,
+                    in1=phase[:, j : j + 1].to_broadcast([P, N_TILE]), op0=ALU.mult, op1=ALU.add,
                 )
                 whole_of[g, j] = whole
 
@@ -312,7 +328,7 @@ def tile_rff_kernel(tc, lt_weight, Lambdas_words, Lambdas_scales, bias, out):
                     home_of[g, part] = home
                 home = home_of[g, part]
                 cols = slice(P * b, P * (b + 1))
-                if s == LAST - 1 or (s == LAST and b % 2 == 0):
+                if s >= LAST - 1 and b % 2 == 0:
                     nc.vector.tensor_scalar_mul(out=home[:, :, cols], in0=upright_of[g, j][:], scalar1=OUT_SCALE)
                 else:
                     nc.scalar.mul(out=home[:, :, cols], in_=upright_of[g, j][:], mul=OUT_SCALE)
@@ -332,7 +348,8 @@ def tile_rff_kernel(tc, lt_weight, Lambdas_words, Lambdas_scales, bias, out):
                 sum_squares_on_vector(t)
             for t in (2, 3, 4, 5, 6, 7):
                 sum_squares_on_scalar(t)
-            clip_factors(0)
+            floor_norms(0, nc.vector)
+            inverse_norms(0)
 
             bias_columns = flipped.tile([P, P], BF16, tag="flip")
             nc.tensor.transpose(bias_columns[:], bias_rows[:], ident_bf[:])
@@ -359,19 +376,20 @@ def tile_rff_kernel(tc, lt_weight, Lambdas_words, Lambdas_scales, bias, out):
                 )
 
             spread_to_phase(0)
+            spread_to_phase(1)
+            clip_factors(0, nc.vector)
             for t in range(GROUP):
                 clip_rows(t)
-            spread_to_phase(1)
             for t in range(GROUP):
                 flip(t, angles, "angle")
             regroup(0, nc.vector.tensor_copy)
-            quantise(0)
+            quantise(0, 1)
             regroup(1, nc.scalar.copy)
-            regroup(3, nc.scalar.copy)
             regroup(2, nc.vector.tensor_copy)
-            for t in (1, 2, 3):
-                quantise(t)
-            clip_factors(1)
+            regroup(3, nc.scalar.copy)
+            quantise(1, 1)
+            quantise(2, PAIR)
+            all_clip_factors(1)
             for t in (8, 9):
                 sum_squares_on_scalar(t)
             clip_rows(4)
@@ -381,7 +399,7 @@ def tile_rff_kernel(tc, lt_weight, Lambdas_words, Lambdas_scales, bias, out):
 
             for k in range(-2, ROW_TILES):
                 if 1 <= k and k % GROUP == 1 and k // GROUP + 2 < GROUPS:
-                    clip_factors(k // GROUP + 2)
+                    all_clip_factors(k // GROUP + 2)
                 run(row_products, k + 1)
                 run(block_factors, k - 2)
                 run(block_sines, k - 1)
@@ -399,8 +417,8 @@ def tile_rff_kernel(tc, lt_weight, Lambdas_words, Lambdas_scales, bias, out):
                     sum_squares_on_scalar(k + 12)
                 if 0 <= k and k + 6 < ROW_TILES and clips_on_scalar(k + 6):
                     clip_rows(k + 6)
-                if GROUP <= k + 4 < ROW_TILES:
-                    quantise(k + 4)
+                if 0 <= k and k + 4 < ROW_TILES and k % PAIR == PAIR - 1:
+                    quantise(k + 4 - (PAIR - 1), PAIR)
                 if 0 <= k and k + 6 < ROW_TILES and not clips_on_scalar(k + 6):
                     clip_rows(k + 6)
                 run(block_products, k + 1)

import math
from contextlib import ExitStack

import concourse.mybir as mybir
from concourse.masks import make_identity

BF16 = mybir.dt.bfloat16
F32 = mybir.dt.float32
I32 = mybir.dt.int32
U32 = mybir.dt.uint32
U8 = mybir.dt.uint8
FP8X4 = mybir.dt.float8_e4m3fn_x4
ACT = mybir.ActivationFunctionType
ALU = mybir.AluOpType

P = 128
PAIR = 2
PACK = 4
HALVES = 2
SIZE, DIM, FDIM = 3072, 512, 2048
ROW_TILES = SIZE // P
GROUP = 4
GROUPS = ROW_TILES // GROUP
GROUP_PAD = 8
N_TILE = 512
ROW_BANKS = 2
ROW_FEATURES = ROW_BANKS * N_TILE
BLOCKS = FDIM // P
SLOT_BLOCKS = (BLOCKS - ROW_FEATURES // P) // GROUP
HOME_BLOCKS = 4
GPSIMD_ROUNDS_FROM = N_TILE
SCALAR_CLIPS_FROM = 18
LAST = ROW_TILES - 1
EPS = 1e-5
MAX_NORM = 1.0 - EPS
TWO_PI = 2.0 * math.pi
ROUND_MAGIC = 1.5 * 2.0**23
OUT_SCALE = math.sqrt(2.0 / DIM)
FLOPS = 2 * SIZE * DIM * FDIM


def tile_rff_kernel(tc, lt_weight, Lambdas_words, Lambdas_scales, bias, out):
    nc = tc.nc
    x_rows = lt_weight.rearrange("(p t) k -> p t k", t=ROW_TILES)
    out_rows = out.rearrange("(p t) n -> p t n", t=ROW_TILES)
    w_hbm = Lambdas_words[0].rearrange("p n t -> p (n t)").bitcast(I32)

    with ExitStack() as ctx:
        keep = ctx.enter_context(tc.tile_pool(name="keep", bufs=1))
        stage = ctx.enter_context(tc.tile_pool(name="stage", bufs=4))
        rounded = ctx.enter_context(tc.tile_pool(name="rounded", bufs=5))
        homes = ctx.enter_context(tc.tile_pool(name="homes", bufs=3))
        flipped = ctx.enter_context(tc.psum_pool(name="flipped", bufs=1))
        angles = ctx.enter_context(tc.psum_pool(name="angles", bufs=5))
        upright = ctx.enter_context(tc.psum_pool(name="upright", bufs=2))

        x_sb = keep.tile([P, ROW_TILES, DIM], BF16)
        w_codes = keep.tile([P, FDIM], U32, align_bytes=64)
        w_plane = keep.tile([P, FDIM], U8, align_bytes=64)
        bias_rows = keep.tile([P, P], BF16)
        bias_row = keep.tile([P, ROW_FEATURES], BF16)
        ones = keep.tile([P, P], BF16)
        row_phase = keep.tile([P, ROW_FEATURES], F32)
        phase = keep.tile([P, BLOCKS], F32)
        phase_rad = keep.tile([P, BLOCKS], F32)
        ident = keep.tile([P, P], F32)
        ident_bf = keep.tile([P, P], BF16)
        minus_half = keep.tile([P, GROUP], F32)
        magic = keep.tile([P, 1], F32)
        warm = keep.tile([P, 1], F32)
        sumsq = keep.tile([P, ROW_TILES], F32)
        floored = keep.tile([P, GROUPS, GROUP_PAD], F32)
        inv_norm = keep.tile([P, GROUPS, GROUP_PAD], F32)
        clip = keep.tile([P, GROUPS, GROUP_PAD], F32)
        e_codes = keep.tile([P, ROW_TILES, P], U32, align_bytes=64)
        e_plane = keep.tile([P, ROW_TILES, P], U8, align_bytes=64)

        nc.vector.memset(bias_rows[:], 0.0)
        nc.vector.memset(minus_half[:], -0.5)
        nc.vector.memset(w_plane[:].bitcast(I32), 0)
        nc.vector.memset(bias_row[:], 0.0)
        nc.vector.memset(ones[:], 1.0)
        nc.vector.memset(magic[:], ROUND_MAGIC)
        make_identity(nc, ident[:])
        make_identity(nc, ident_bf[:])

        nc.scalar.dma_start(out=bias_rows[0:BLOCKS, :], in_=bias.rearrange("(j p) -> j p", p=P))
        nc.scalar.dma_start(out=bias_row[0:1, :], in_=bias[0:ROW_FEATURES].unsqueeze(0))
        nc.scalar.activation(out=warm[:], in_=minus_half[:, 0:1], func=ACT.Sin)

        def load_group(g):
            nc.sync.dma_start(
                out=x_sb[:, GROUP * g : GROUP * (g + 1), :], in_=x_rows[:, GROUP * g : GROUP * (g + 1), :]
            )

        load_group(0)
        for q in range(4):
            nc.sync.dma_start(
                out=w_plane[32 * q : 32 * q + 4, :].bitcast(I32),
                in_=Lambdas_scales[0, 4 * q : 4 * q + 4, :].bitcast(I32),
            )

        def load_weight(first, count):
            cols = slice(first, first + count)
            nc.sync.dma_start(out=w_codes[:, cols].bitcast(I32), in_=w_hbm[:, cols])

        load_weight(0, ROW_FEATURES)
        load_group(1)
        load_weight(ROW_FEATURES, FDIM - ROW_FEATURES)
        for g in range(2, GROUPS):
            load_group(g)

        e_of = {}
        flipped_of = {}
        grouped_of = {}
        angles_of = {}
        turns_of = {}
        shifted_of = {}
        part_of = {}
        sine_of = {}
        whole_of = {}
        block_part_of = {}
        block_sine_of = {}
        upright_of = {}
        home_of = {}

        def sum_squares_on_scalar(t):
            squares = stage.tile([P, DIM], BF16)
            nc.scalar.activation(
                out=squares[:], in_=x_sb[:, t, :], func=ACT.Square, accum_out=sumsq[:, t : t + 1]
            )

        def sum_squares_on_vector(t):
            products = stage.tile([P, DIM], F32)
            nc.vector.scalar_tensor_tensor(
                out=products[:], in0=x_sb[:, t, :], scalar=1.0, in1=x_sb[:, t, :],
                op0=ALU.mult, op1=ALU.mult, accum_out=sumsq[:, t : t + 1],
            )

        def floor_norms(g, engine):
            engine.tensor_scalar(
                out=floored[:, g, 0:GROUP], in0=sumsq[:, GROUP * g : GROUP * (g + 1)], scalar1=EPS * EPS,
                scalar2=0.0, op0=ALU.max, op1=ALU.add,
            )

        def inverse_norms(g):
            nc.gpsimd.tensor_tensor(
                out=inv_norm[:, g, 0:GROUP], in0=floored[:, g, 0:GROUP], in1=minus_half[:], op=ALU.pow
            )

        def clip_factors(g, engine):
            engine.tensor_scalar(
                out=clip[:, g, 0:GROUP], in0=inv_norm[:, g, 0:GROUP], scalar1=MAX_NORM, scalar2=1.0,
                op0=ALU.mult, op1=ALU.min,
            )

        def all_clip_factors(g):
            floor_norms(g, nc.gpsimd)
            inverse_norms(g)
            clip_factors(g, nc.gpsimd)

        def clip_rows(t):
            g, i = divmod(t, GROUP)
            factor = clip[:, g, i : i + 1]
            e_sb = stage.tile([P, DIM], BF16)
            if clips_on_scalar(t):
                nc.scalar.activation(out=e_sb[:], in_=x_sb[:, t, :], func=ACT.Copy, scale=factor)
            else:
                nc.vector.tensor_scalar_mul(out=e_sb[:], in0=x_sb[:, t, :], scalar1=factor)
            e_of[t] = e_sb

        def clips_on_scalar(t):
            return t in (GROUP, GROUP + 1) or t >= SCALAR_CLIPS_FROM

        def flip(t, pool, tag):
            e_words = e_of[t][:].bitcast(F32)
            e_t = pool.tile([P, HALVES, P], F32, tag=tag)
            for u in range(HALVES):
                nc.tensor.transpose(e_t[:, u, :], e_words[:, u : DIM // 2 : HALVES], ident[:])
            flipped_of[t] = e_t

        def regroup(t, copy_words):
            if t % PAIR == 0:
                grouped = stage.tile([P, PAIR, P * PACK], BF16, align_bytes=64)
                grouped_of[t // PAIR] = grouped
            copy_words(
                out=grouped_of[t // PAIR][:, t % PAIR, :].bitcast(F32),
                in_=flipped_of[t][:].rearrange("p u r -> p r u"),
            )

        def quantise(t, count):
            some = slice(t % PAIR, t % PAIR + count)
            codes, plane = e_side(t, count)
            nc.vector.quantize_mx(
                out=codes, scales=plane, in_=grouped_of[t // PAIR][:, some, :].rearrange("p t r -> p (t r)")
            )

        def e_side(first, count):
            rows = slice(first, first + count)
            return (
                e_codes[:, rows, :].rearrange("p t r -> p (t r)").bitcast(FP8X4),
                e_plane[:, rows, :].rearrange("p t r -> p (t r)"),
            )

        def w_side(first, count):
            cols = slice(first, first + count)
            return w_codes[:, cols].bitcast(FP8X4), w_plane[:, cols]

        def product(key, still, moving):
            angle = angles.tile([P, N_TILE], F32, tag="angle")
            nc.tensor.matmul_mx(
                out=angle[:], lhsT=still[0], lhsT_scale=still[1], rhs=moving[0], rhs_scale=moving[1],
                start=True, stop=True,
            )
            angles_of[key] = angle

        def row_products(t):
            for n in range(ROW_BANKS):
                product(("row", t, n), e_side(t, 1), w_side(N_TILE * n, N_TILE))

        def row_turns(t):
            turns = stage.tile([P, ROW_FEATURES], F32)
            for n in range(ROW_BANKS):
                cols = slice(N_TILE * n, N_TILE * (n + 1))
                nc.vector.scalar_tensor_tensor(
                    out=turns[:, cols], in0=angles_of["row", t, n][:], scalar=1.0 / TWO_PI,
                    in1=row_phase[:, cols], op0=ALU.mult, op1=ALU.add,
                )
            turns_of[t] = turns

        def round_on_scalar(t):
            cols = slice(0, ROW_FEATURES if t == LAST else GPSIMD_ROUNDS_FROM)
            shifted = rounded.tile([P, ROW_FEATURES], F32)
            nc.scalar.activation(
                out=shifted[:, cols], in_=turns_of[t][:, cols], func=ACT.Identity, bias=magic[:]
            )
            shifted_of[t] = shifted

        def round_on_gpsimd(t):
            nc.gpsimd.tensor_scalar(
                out=shifted_of[t][:, GPSIMD_ROUNDS_FROM:], in0=turns_of[t][:, GPSIMD_ROUNDS_FROM:],
                scalar1=1.0, scalar2=ROUND_MAGIC, op0=ALU.mult, op1=ALU.add,
            )

        def fraction(t):
            neg_frac = stage.tile([P, ROW_FEATURES], F32)
            nc.vector.scalar_tensor_tensor(
                out=neg_frac[:], in0=shifted_of[t][:], scalar=ROUND_MAGIC, in1=turns_of[t][:],
                op0=ALU.subtract, op1=ALU.subtract,
            )
            part_of[t] = neg_frac

        def row_pieces(t):
            width = N_TILE if t >= LAST - 1 else ROW_FEATURES
            return [slice(n0, n0 + width) for n0 in range(0, ROW_FEATURES, width)]

        def row_sine(t):
            sin_row = stage.tile([P, ROW_FEATURES], F32)
            for cols in row_pieces(t):
                nc.scalar.activation(
                    out=sin_row[:, cols], in_=part_of[t][:, cols], func=ACT.Sin, scale=-TWO_PI
                )
            sine_of[t] = sin_row

        def row_factor(t):
            row_home = shifted_of[t + 2] if t < LAST - 3 else sine_of[t]
            for cols in row_pieces(t):
                if t == LAST:
                    nc.vector.tensor_scalar_mul(
                        out=row_home[:, cols], in0=sine_of[t][:, cols], scalar1=OUT_SCALE
                    )
                else:
                    nc.gpsimd.tensor_scalar(
                        out=row_home[:, cols], in0=sine_of[t][:, cols], scalar1=OUT_SCALE, scalar2=0.0,
                        op0=ALU.mult, op1=ALU.add,
                    )
                nc.sync.dma_start(out=out_rows[:, t, cols], in_=row_home[:, cols])

        def blocks_of(s):
            g, i = divmod(s, GROUP)
            first = ROW_FEATURES // P + SLOT_BLOCKS * i
            return [(g, j) for j in range(first, first + SLOT_BLOCKS)]

        def block_products(s):
            for g, j in blocks_of(s):
                product((g, j), w_side(P * j, P), e_side(GROUP * g, GROUP))

        def whole_turns(s):
            for g, j in blocks_of(s):
                whole = stage.tile([P, N_TILE], I32)
                nc.vector.scalar_tensor_tensor(
                    out=whole[:], in0=angles_of[g, j][:], scalar=1.0 / TWO_PI,
                    in1=phase[:, j : j + 1].to_broadcast([P, N_TILE]), op0=ALU.mult, op1=ALU.add,
                )
                whole_of[g, j] = whole

        def part_turns(s):
            for g, j in blocks_of(s):
                block_part = stage.tile([P, N_TILE], F32)
                nc.vector.scalar_tensor_tensor(
                    out=block_part[:], in0=angles_of[g, j][:], scalar=1.0 / TWO_PI, in1=whole_of[g, j][:],
                    op0=ALU.mult, op1=ALU.subtract,
                )
                block_part_of[g, j] = block_part

        def block_sines(s):
            for g, j in blocks_of(s):
                block_sine = stage.tile([P, N_TILE], F32)
                nc.scalar.activation(
                    out=block_sine[:], in_=block_part_of[g, j][:], func=ACT.Sin, scale=TWO_PI,
                    bias=phase_rad[:, j : j + 1],
                )
                block_sine_of[g, j] = block_sine

        def turn_back(s):
            for g, j in blocks_of(s):
                pool, tag = (angles, "angle") if s == LAST else (upright, "up")
                up = pool.tile([P, GROUP, P], F32, tag=tag)
                for i in range(GROUP):
                    nc.tensor.transpose(up[:, i, :], block_sine_of[g, j][:, P * i : P * (i + 1)], ident[:])
                upright_of[g, j] = up

        def block_factors(s):
            for g, j in blocks_of(s):
                part, b = divmod(j, HOME_BLOCKS)
                if b == 0:
                    home = homes.tile([P, GROUP, HOME_BLOCKS * P], F32)
                    home_of[g, part] = home
                home = home_of[g, part]
                cols = slice(P * b, P * (b + 1))
                if s >= LAST - 1 and b % 2 == 0:
                    nc.vector.tensor_scalar_mul(out=home[:, :, cols], in0=upright_of[g, j][:], scalar1=OUT_SCALE)
                else:
                    nc.scalar.mul(out=home[:, :, cols], in_=upright_of[g, j][:], mul=OUT_SCALE)
                rows = slice(GROUP * g, GROUP * (g + 1))
                if s >= LAST - 1:
                    nc.sync.dma_start(out=out_rows[:, rows, P * j : P * (j + 1)], in_=home[:, :, cols])
                elif b == HOME_BLOCKS - 1:
                    first = HOME_BLOCKS * P * part
                    nc.sync.dma_start(out=out_rows[:, rows, first : first + HOME_BLOCKS * P], in_=home[:])

        def run(stage_of, s):
            if 0 <= s < ROW_TILES:
                stage_of(s)

        with tc.manual_schedule():
            for t in (0, 1):
                sum_squares_on_vector(t)
            for t in (2, 3, 4, 5, 6, 7):
                sum_squares_on_scalar(t)
            floor_norms(0, nc.vector)
            inverse_norms(0)

            bias_columns = flipped.tile([P, P], BF16, tag="flip")
            nc.tensor.transpose(bias_columns[:], bias_rows[:], ident_bf[:])
            nc.vector.tensor_scalar(
                out=phase[:], in0=bias_columns[:, 0:BLOCKS], scalar1=1.0 / TWO_PI, scalar2=0.25,
                op0=ALU.mult, op1=ALU.add,
            )
            nc.vector.tensor_scalar(
                out=phase_rad[:], in0=bias_columns[:, 0:BLOCKS], scalar1=1.0, scalar2=0.5 * math.pi,
                op0=ALU.mult, op1=ALU.add,
            )
            spreads = []
            for n0 in range(0, ROW_FEATURES, N_TILE):
                spread = upright.tile([P, N_TILE], F32, tag="up")
                nc.tensor.matmul(
                    out=spread[:], lhsT=ones[:], rhs=bias_row[:, n0 : n0 + N_TILE], start=True, stop=True
                )
                spreads.append(spread)

            def spread_to_phase(n):
                nc.vector.tensor_scalar(
                    out=row_phase[:, N_TILE * n : N_TILE * (n + 1)], in0=spreads[n][:],
                    scalar1=1.0 / TWO_PI, scalar2=0.25, op0=ALU.mult, op1=ALU.add,
                )

            spread_to_phase(0)
            spread_to_phase(1)
            clip_factors(0, nc.vector)
            for t in range(GROUP):
                clip_rows(t)
            for t in range(GROUP):
                flip(t, angles, "angle")
            regroup(0, nc.vector.tensor_copy)
            quantise(0, 1)
            regroup(1, nc.scalar.copy)
            regroup(2, nc.vector.tensor_copy)
            regroup(3, nc.scalar.copy)
            quantise(1, 1)
            quantise(2, PAIR)
            all_clip_factors(1)
            for t in (8, 9):
                sum_squares_on_scalar(t)
            clip_rows(4)
            for t in (10, 11):
                sum_squares_on_scalar(t)
            clip_rows(5)

            for k in range(-2, ROW_TILES):
                if 1 <= k and k % GROUP == 1 and k // GROUP + 2 < GROUPS:
                    all_clip_factors(k // GROUP + 2)
                run(row_products, k + 1)
                run(block_factors, k - 2)
                run(block_sines, k - 1)
                run(turn_back, k - 1)
                if k >= 0 and k + 5 < ROW_TILES:
                    flip(k + 5, flipped, "flip")
                run(row_turns, k)
                run(whole_turns, k)
                run(part_turns, k)
                if GROUP <= k + 4 < ROW_TILES:
                    regroup(k + 4, nc.scalar.copy)
                run(row_sine, k - 2)
                run(round_on_scalar, k)
                if 0 <= k < ROW_TILES - 12:
                    sum_squares_on_scalar(k + 12)
                if 0 <= k and k + 6 < ROW_TILES and clips_on_scalar(k + 6):
                    clip_rows(k + 6)
                if 0 <= k and k + 4 < ROW_TILES and k % PAIR == PAIR - 1:
                    quantise(k + 4 - (PAIR - 1), PAIR)
                if 0 <= k and k + 6 < ROW_TILES and not clips_on_scalar(k + 6):
                    clip_rows(k + 6)
                run(block_products, k + 1)
                if k == -1:
                    flip(GROUP, flipped, "flip")
                run(fraction, k - 1)
                run(row_factor, k - 3)
                if 0 <= k < LAST:
                    round_on_gpsimd(k)

            row_factor(LAST - 2)
            fraction(LAST)
            block_sines(LAST)
            turn_back(LAST)
            row_sine(LAST - 1)
            row_factor(LAST - 1)
            block_factors(LAST - 1)
            row_sine(LAST)
            block_factors(LAST)
            row_factor(LAST)
